import numpy as np
import ml_dtypes


def mxq(x, axis, fmt="e4m3"):
    dtype, down = {"e4m3": (ml_dtypes.float8_e4m3fn, 7), "e5m2": (ml_dtypes.float8_e5m2, 14)}[fmt]
    v = np.moveaxis(np.asarray(x, np.float32).astype(ml_dtypes.bfloat16).astype(np.float64), axis, -1)
    blocks = v.reshape(v.shape[:-1] + (-1, 32))
    amax = np.abs(blocks).max(-1, keepdims=True)
    byte = np.maximum(np.where(amax > 0, np.frexp(amax)[1] - 1 + 127, 0) - down, 1)
    scale = np.exp2(byte - 127.0)
    codes = (blocks / scale).astype(np.float32).astype(dtype).astype(np.float64)
    return np.moveaxis((codes * scale).reshape(v.shape), -1, axis)


WIDE = False


def mx_kscale(k):
    if not WIDE:
        return np.ones(k)
    levels = np.array([10, -10, 5, -5, 0])
    a = np.random.permutation(np.resize(levels, k // 512 * 4)).reshape(k // 512, 4)
    idx = np.arange(k)
    return np.exp2(a[idx // 512, idx % 128 // 32])


BF16 = ml_dtypes.bfloat16


def bf(x):
    return np.asarray(x, np.float32).astype(BF16)


def f64(x):
    return np.asarray(x).astype(np.float64)


S, B, D0, D1, D2, O = 32, 128, 512, 512, 512, 128


def sample(eps, logvar, mean):
    return eps * np.exp(0.5 * logvar) + mean


def setup_inputs():
    s = mx_kscale(D1)
    return {
        "h0": bf(np.maximum(np.random.standard_normal((S, B, D1)), 0.0) * 1.1 * s),
        "wm1": bf(np.random.standard_normal((D1, D2)) * 0.8 / np.sqrt(D1) / s[:, None]),
        "wv1": bf(2.0 * np.log(0.6 / np.sqrt(D1)) + 0.5 * np.random.standard_normal((D1, D2))),
        "bm1": bf(np.random.standard_normal(D2) * 0.3),
        "bv1": bf(2.0 * np.log(0.3) + 0.5 * np.random.standard_normal(D2)),
        "we1": bf(np.random.standard_normal((S, D1, D2)) / s[None, :, None]),
        "be1": bf(np.random.standard_normal((S, 1, D2))),
    }


def reference(h0, wm1, wv1, bm1, bv1, we1, be1):
    w1 = sample(f64(we1), f64(wv1), f64(wm1))
    b1 = sample(f64(be1), f64(bv1), f64(bm1))
    return np.maximum((mxq(f64(h0), 2, "e4m3") @ mxq(w1, 1, "e4m3")) + b1, 0.0)

@@ -1,0 +1,158 @@
+from contextlib import ExitStack
+
+import concourse.mybir as mybir
+from concourse.masks import make_identity
+
+BF16 = mybir.dt.bfloat16
+F32 = mybir.dt.float32
+U32 = mybir.dt.uint32
+U8 = mybir.dt.uint8
+FP8X4 = mybir.dt.float8_e4m3fn_x4
+ACT = mybir.ActivationFunctionType
+ALU = mybir.AluOpType
+
+SAMPLES = 32
+ROWS = 128
+K = 512
+N = 512
+P = 128
+PACK = 4
+SLICES = N // P
+PAIR = 2
+
+FLOPS = 2 * SAMPLES * ROWS * K * N
+
+
+def tile_bnn_pb_kernel(tc, h0, wm1, wv1, bm1, bv1, we1, be1, out):
+    nc = tc.nc
+    with ExitStack() as ctx:
+        const = ctx.enter_context(tc.tile_pool(name="const", bufs=1))
+        loads = ctx.enter_context(tc.tile_pool(name="loads", bufs=3))
+        work = ctx.enter_context(tc.tile_pool(name="work", bufs=2))
+        packed = ctx.enter_context(tc.tile_pool(name="packed", bufs=3))
+        results = ctx.enter_context(tc.tile_pool(name="results", bufs=3))
+        psum_setup = ctx.enter_context(tc.psum_pool(name="psum_setup", bufs=1))
+        psum = ctx.enter_context(tc.psum_pool(name="psum", bufs=2))
+
+        ident_f32 = const.tile([P, P], F32)
+        make_identity(nc, ident_f32[:])
+        ident_bf16 = const.tile([P, P], BF16)
+        make_identity(nc, ident_bf16[:])
+
+        logvar_rows = const.tile([P, PACK, N], BF16)
+        nc.sync.dma_start(out=logvar_rows[:], in_=wv1.rearrange("(p t) n -> p t n", t=PACK))
+        mean_rows = const.tile([P, PACK, N], BF16)
+        nc.sync.dma_start(out=mean_rows[:], in_=wm1.rearrange("(p t) n -> p t n", t=PACK))
+        sigma = const.tile([P, N, PACK], F32)
+        nc.scalar.activation(
+            out=sigma[:], in_=logvar_rows[:].rearrange("p t n -> p n t"), func=ACT.Exp, scale=0.5
+        )
+        mean = const.tile([P, N, PACK], BF16)
+        nc.vector.tensor_copy(out=mean[:], in_=mean_rows[:].rearrange("p t n -> p n t"))
+
+        bias_noise_rows = const.tile([P, P], BF16)
+        nc.sync.dma_start(out=bias_noise_rows[:], in_=be1.rearrange("s o (c l) -> (s o c) l", l=P))
+        bias_stat_rows = const.tile([P, P], BF16)
+        nc.vector.memset(bias_stat_rows[:], 0.0)
+        nc.sync.dma_start(out=bias_stat_rows[0:SLICES, :], in_=bv1.rearrange("(c l) -> c l", l=P))
+        nc.sync.dma_start(
+            out=bias_stat_rows[SLICES : 2 * SLICES, :], in_=bm1.rearrange("(c l) -> c l", l=P)
+        )
+        bias_noise = psum_setup.tile([P, P], BF16)
+        nc.tensor.transpose(bias_noise[:], bias_noise_rows[:], ident_bf16[:])
+        bias_stat = psum_setup.tile([P, P], BF16)
+        nc.tensor.transpose(bias_stat[:], bias_stat_rows[:], ident_bf16[:])
+        bias_sigma = const.tile([P, SLICES], F32)
+        nc.scalar.activation(out=bias_sigma[:], in_=bias_stat[:, 0:SLICES], func=ACT.Exp, scale=0.5)
+        bias_mean = const.tile([P, SLICES], F32)
+        nc.scalar.copy(out=bias_mean[:], in_=bias_stat[:, SLICES : 2 * SLICES])
+        bias_scaled = const.tile([P, SAMPLES, SLICES], F32)
+        nc.vector.tensor_tensor(
+            out=bias_scaled[:],
+            in0=bias_noise[:].rearrange("l (s c) -> l s c", c=SLICES),
+            in1=bias_sigma[:].unsqueeze(1).to_broadcast([P, SAMPLES, SLICES]),
+            op=ALU.mult,
+        )
+        bias = const.tile([P, SAMPLES, SLICES], F32)
+        nc.vector.tensor_tensor(
+            out=bias[:],
+            in0=bias_scaled[:],
+            in1=bias_mean[:].unsqueeze(1).to_broadcast([P, SAMPLES, SLICES]),
+            op=ALU.add,
+        )
+
+        for first in range(0, SAMPLES, PAIR):
+            pair = slice(first, first + PAIR)
+
+            noise = loads.tile([P, PAIR, PACK, N], BF16)
+            nc.sync.dma_start(out=noise[:], in_=we1[pair].rearrange("s (p t) n -> p s t n", t=PACK))
+            scaled = work.tile([P, PAIR, N, PACK], F32)
+            nc.vector.tensor_tensor(
+                out=scaled[:],
+                in0=noise[:].rearrange("p s t n -> p s n t"),
+                in1=sigma[:].unsqueeze(1).to_broadcast([P, PAIR, N, PACK]),
+                op=ALU.mult,
+            )
+            weights = work.tile([P, PAIR, N, PACK], BF16, align_bytes=64)
+            nc.vector.tensor_tensor(
+                out=weights[:],
+                in0=scaled[:],
+                in1=mean[:].unsqueeze(1).to_broadcast([P, PAIR, N, PACK]),
+                op=ALU.add,
+            )
+            w_codes = packed.tile([P, PAIR * N], U32, align_bytes=64)
+            w_scales = packed.tile([P, PAIR * N], U8, align_bytes=64)
+            nc.vector.quantize_mx(
+                out=w_codes[:].bitcast(FP8X4),
+                scales=w_scales[:],
+                in_=weights[:].rearrange("p s n t -> p (s n t)"),
+            )
+
+            acts = loads.tile([P, PAIR, K], BF16)
+            nc.sync.dma_start(out=acts[:], in_=h0[pair].rearrange("s r k -> r s k"))
+            act_words = acts[:].bitcast(F32).rearrange("r s (q u) -> r s u q", u=2)
+            turned = psum.tile([P, PAIR, 2, ROWS], F32)
+            for j in range(PAIR):
+                for u in range(2):
+                    nc.tensor.transpose(turned[:, j, u, :], act_words[:, j, u, :], ident_f32[:])
+            grouped = work.tile([P, PAIR, ROWS, PACK], BF16, align_bytes=64)
+            nc.scalar.copy(
+                out=grouped[:].bitcast(F32), in_=turned[:].rearrange("q s u r -> q s r u")
+            )
+            h_codes = packed.tile([P, PAIR * ROWS], U32, align_bytes=64)
+            h_scales = packed.tile([P, PAIR * ROWS], U8, align_bytes=64)
+            nc.vector.quantize_mx(
+                out=h_codes[:].bitcast(FP8X4),
+                scales=h_scales[:],
+                in_=grouped[:].rearrange("q s r t -> q (s r t)"),
+            )
+
+            result = results.tile([P, PAIR, N], F32)
+            for j in range(PAIR):
+                rows = slice(j * ROWS, (j + 1) * ROWS)
+                product = psum.tile([P, SLICES, ROWS], F32)
+                for c in range(SLICES):
+                    cols = slice(j * N + c * P, j * N + (c + 1) * P)
+                    nc.tensor.matmul_mx(
+                        out=product[:, c, :],
+                        lhsT=w_codes[:, cols].bitcast(FP8X4),
+                        lhsT_scale=w_scales[:, cols],
+                        rhs=h_codes[:, rows].bitcast(FP8X4),
+                        rhs_scale=h_scales[:, rows],
+                        start=True,
+                        stop=True,
+                    )
+                hidden = results.tile([P, SLICES, ROWS], F32)
+                for c in range(SLICES):
+                    nc.scalar.activation(
+                        out=hidden[:, c, :],
+                        in_=product[:, c, :],
+                        func=ACT.Relu,
+                        bias=bias[:, first + j, c : c + 1],
+                        scale=1.0,
+                    )
+                back = psum.tile([P, SLICES, P], F32)
+                for c in range(SLICES):
+                    nc.tensor.transpose(back[:, c, :], hidden[:, c, :], ident_f32[:])
+                nc.scalar.copy(out=result[:, j, :], in_=back[:].rearrange("r c l -> r (c l)"))
+            nc.scalar.dma_start(out=out[pair].rearrange("s r n -> r s n"), in_=result[:])

@@ -18,7 +18,9 @@ N = 512
 P = 128
 PACK = 4
 SLICES = N // P
-PAIR = 2
+GROUP = 3
+F32_BANK_N = 512 // PACK
+BF16_BANK_N = 1024 // PACK
 
 FLOPS = 2 * SAMPLES * ROWS * K * N
 
@@ -31,7 +33,7 @@ def tile_bnn_pb_kernel(tc, h0, wm1, wv1, bm1, bv1, we1, be1, out):
         work = ctx.enter_context(tc.tile_pool(name="work", bufs=2))
         packed = ctx.enter_context(tc.tile_pool(name="packed", bufs=3))
         results = ctx.enter_context(tc.tile_pool(name="results", bufs=3))
-        psum_setup = ctx.enter_context(tc.psum_pool(name="psum_setup", bufs=1))
+        psum_const = ctx.enter_context(tc.psum_pool(name="psum_const", bufs=1))
         psum = ctx.enter_context(tc.psum_pool(name="psum", bufs=2))
 
         ident_f32 = const.tile([P, P], F32)
@@ -44,11 +46,38 @@ def tile_bnn_pb_kernel(tc, h0, wm1, wv1, bm1, bv1, we1, be1, out):
         mean_rows = const.tile([P, PACK, N], BF16)
         nc.sync.dma_start(out=mean_rows[:], in_=wm1.rearrange("(p t) n -> p t n", t=PACK))
         sigma = const.tile([P, N, PACK], F32)
-        nc.scalar.activation(
-            out=sigma[:], in_=logvar_rows[:].rearrange("p t n -> p n t"), func=ACT.Exp, scale=0.5
-        )
+        sigma_banks = []
+        for n0 in range(0, N, F32_BANK_N):
+            cols = slice(n0, n0 + F32_BANK_N)
+            nc.scalar.activation(
+                out=sigma[:, cols, :],
+                in_=logvar_rows[:, :, cols].rearrange("p t n -> p n t"),
+                func=ACT.Exp,
+                scale=0.5,
+            )
+            bank = psum_const.tile([P, F32_BANK_N, PACK], F32, name="sigma_bank%d" % n0)
+            nc.tensor.matmul(
+                out=bank[:].rearrange("p n t -> p (n t)"),
+                lhsT=ident_f32[:],
+                rhs=sigma[:, cols, :].rearrange("p n t -> p (n t)"),
+                start=True,
+                stop=True,
+            )
+            sigma_banks.append(bank)
         mean = const.tile([P, N, PACK], BF16)
         nc.vector.tensor_copy(out=mean[:], in_=mean_rows[:].rearrange("p t n -> p n t"))
+        mean_banks = []
+        for n0 in range(0, N, BF16_BANK_N):
+            bank = psum_const.tile([P, BF16_BANK_N, PACK], BF16, name="mean_bank%d" % n0)
+            for half in range(0, BF16_BANK_N, F32_BANK_N):
+                nc.tensor.matmul(
+                    out=bank[:, half : half + F32_BANK_N, :].rearrange("p n t -> p (n t)"),
+                    lhsT=ident_bf16[:],
+                    rhs=mean[:, n0 + half : n0 + half + F32_BANK_N, :].rearrange("p n t -> p (n t)"),
+                    start=True,
+                    stop=True,
+                )
+            mean_banks.append(bank)
 
         bias_noise_rows = const.tile([P, P], BF16)
         nc.sync.dma_start(out=bias_noise_rows[:], in_=be1.rearrange("s o (c l) -> (s o c) l", l=P))
@@ -58,9 +87,9 @@ def tile_bnn_pb_kernel(tc, h0, wm1, wv1, bm1, bv1, we1, be1, out):
         nc.sync.dma_start(
             out=bias_stat_rows[SLICES : 2 * SLICES, :], in_=bm1.rearrange("(c l) -> c l", l=P)
         )
-        bias_noise = psum_setup.tile([P, P], BF16)
+        bias_noise = psum.tile([P, P], BF16, tag="bank")
         nc.tensor.transpose(bias_noise[:], bias_noise_rows[:], ident_bf16[:])
-        bias_stat = psum_setup.tile([P, P], BF16)
+        bias_stat = psum.tile([P, P], BF16, tag="bank")
         nc.tensor.transpose(bias_stat[:], bias_stat_rows[:], ident_bf16[:])
         bias_sigma = const.tile([P, SLICES], F32)
         nc.scalar.activation(out=bias_sigma[:], in_=bias_stat[:, 0:SLICES], func=ACT.Exp, scale=0.5)
@@ -81,64 +110,82 @@ def tile_bnn_pb_kernel(tc, h0, wm1, wv1, bm1, bv1, we1, be1, out):
             op=ALU.add,
         )
 
-        for first in range(0, SAMPLES, PAIR):
-            pair = slice(first, first + PAIR)
+        for first in range(0, SAMPLES, GROUP):
+            count = min(GROUP, SAMPLES - first)
+            on_vector = min(GROUP - 1, count)
+            group = slice(first, first + count)
 
-            noise = loads.tile([P, PAIR, PACK, N], BF16)
-            nc.sync.dma_start(out=noise[:], in_=we1[pair].rearrange("s (p t) n -> p s t n", t=PACK))
-            scaled = work.tile([P, PAIR, N, PACK], F32)
-            nc.vector.tensor_tensor(
-                out=scaled[:],
-                in0=noise[:].rearrange("p s t n -> p s n t"),
-                in1=sigma[:].unsqueeze(1).to_broadcast([P, PAIR, N, PACK]),
-                op=ALU.mult,
+            noise = loads.tile([P, GROUP, PACK, N], BF16)
+            nc.sync.dma_start(
+                out=noise[:, 0:count], in_=we1[group].rearrange("s (p t) n -> p s t n", t=PACK)
             )
-            weights = work.tile([P, PAIR, N, PACK], BF16, align_bytes=64)
-            nc.vector.tensor_tensor(
-                out=weights[:],
-                in0=scaled[:],
-                in1=mean[:].unsqueeze(1).to_broadcast([P, PAIR, N, PACK]),
-                op=ALU.add,
-            )
-            w_codes = packed.tile([P, PAIR * N], U32, align_bytes=64)
-            w_scales = packed.tile([P, PAIR * N], U8, align_bytes=64)
-            nc.vector.quantize_mx(
-                out=w_codes[:].bitcast(FP8X4),
-                scales=w_scales[:],
-                in_=weights[:].rearrange("p s n t -> p (s n t)"),
-            )
+            acts = loads.tile([P, GROUP, K], BF16)
+            nc.sync.dma_start(out=acts[:, 0:count], in_=h0[group].rearrange("s r k -> r s k"))
+            noise_nt = noise[:].rearrange("p s t n -> p s n t")
+            weights = work.tile([P, GROUP, N, PACK], BF16, align_bytes=64)
 
-            acts = loads.tile([P, PAIR, K], BF16)
-            nc.sync.dma_start(out=acts[:], in_=h0[pair].rearrange("s r k -> r s k"))
+            if count == GROUP:
+                scaled_g = work.tile([P, N, PACK], F32)
+                nc.gpsimd.tensor_tensor(
+                    out=scaled_g[:], in0=noise_nt[:, GROUP - 1], in1=sigma[:], op=ALU.mult
+                )
+                nc.gpsimd.tensor_tensor(
+                    out=weights[:, GROUP - 1], in0=scaled_g[:], in1=mean[:], op=ALU.add
+                )
+
+            scaled_v = work.tile([P, GROUP - 1, N, PACK], F32)
+            for i, bank in enumerate(sigma_banks):
+                cols = slice(i * F32_BANK_N, (i + 1) * F32_BANK_N)
+                nc.vector.tensor_tensor(
+                    out=scaled_v[:, 0:on_vector, cols, :],
+                    in0=noise_nt[:, 0:on_vector, cols, :],
+                    in1=bank[:].unsqueeze(1).to_broadcast([P, on_vector, F32_BANK_N, PACK]),
+                    op=ALU.mult,
+                )
+            for i, bank in enumerate(mean_banks):
+                cols = slice(i * BF16_BANK_N, (i + 1) * BF16_BANK_N)
+                nc.vector.tensor_tensor(
+                    out=weights[:, 0:on_vector, cols, :],
+                    in0=scaled_v[:, 0:on_vector, cols, :],
+                    in1=bank[:].unsqueeze(1).to_broadcast([P, on_vector, BF16_BANK_N, PACK]),
+                    op=ALU.add,
+                )
+
             act_words = acts[:].bitcast(F32).rearrange("r s (q u) -> r s u q", u=2)
-            turned = psum.tile([P, PAIR, 2, ROWS], F32)
-            for j in range(PAIR):
+            h_codes = packed.tile([P, GROUP, ROWS], U32, align_bytes=64)
+            h_scales = packed.tile([P, GROUP, ROWS], U8, align_bytes=64)
+            for j in range(count):
+                turned = psum.tile([P, 2, ROWS], F32, tag="bank")
                 for u in range(2):
-                    nc.tensor.transpose(turned[:, j, u, :], act_words[:, j, u, :], ident_f32[:])
-            grouped = work.tile([P, PAIR, ROWS, PACK], BF16, align_bytes=64)
-            nc.scalar.copy(
-                out=grouped[:].bitcast(F32), in_=turned[:].rearrange("q s u r -> q s r u")
-            )
-            h_codes = packed.tile([P, PAIR * ROWS], U32, align_bytes=64)
-            h_scales = packed.tile([P, PAIR * ROWS], U8, align_bytes=64)
-            nc.vector.quantize_mx(
-                out=h_codes[:].bitcast(FP8X4),
-                scales=h_scales[:],
-                in_=grouped[:].rearrange("q s r t -> q (s r t)"),
-            )
+                    nc.tensor.transpose(turned[:, u, :], act_words[:, j, u, :], ident_f32[:])
+                grouped = work.tile([P, ROWS, PACK], BF16, align_bytes=64)
+                nc.scalar.copy(out=grouped[:].bitcast(F32), in_=turned[:].rearrange("q u r -> q r u"))
+                nc.vector.quantize_mx(
+                    out=h_codes[:, j, :].bitcast(FP8X4),
+                    scales=h_scales[:, j, :],
+                    in_=grouped[:].rearrange("q r t -> q (r t)"),
+                )
 
-            result = results.tile([P, PAIR, N], F32)
-            for j in range(PAIR):
-                rows = slice(j * ROWS, (j + 1) * ROWS)
-                product = psum.tile([P, SLICES, ROWS], F32)
+            w_codes = packed.tile([P, GROUP, N], U32, align_bytes=64)
+            w_scales = packed.tile([P, GROUP, N], U8, align_bytes=64)
+            for j in range(count):
+                nc.vector.quantize_mx(
+                    out=w_codes[:, j, :].bitcast(FP8X4),
+                    scales=w_scales[:, j, :],
+                    in_=weights[:, j].rearrange("p n t -> p (n t)"),
+                )
+
+            result = results.tile([P, GROUP, N], F32)
+            for j in range(count):
+                product = psum.tile([P, SLICES, ROWS], F32, tag="bank")
                 for c in range(SLICES):
-                    cols = slice(j * N + c * P, j * N + (c + 1) * P)
+                    cols = slice(c * P, (c + 1) * P)
                     nc.tensor.matmul_mx(
                         out=product[:, c, :],
-                        lhsT=w_codes[:, cols].bitcast(FP8X4),
-                        lhsT_scale=w_scales[:, cols],
-                        rhs=h_codes[:, rows].bitcast(FP8X4),
-                        rhs_scale=h_scales[:, rows],
+                        lhsT=w_codes[:, j, cols].bitcast(FP8X4),
+                        lhsT_scale=w_scales[:, j, cols],
+                        rhs=h_codes[:, j, :].bitcast(FP8X4),
+                        rhs_scale=h_scales[:, j, :],
                         start=True,
                         stop=True,
                     )
@@ -151,8 +198,10 @@ def tile_bnn_pb_kernel(tc, h0, wm1, wv1, bm1, bv1, we1, be1, out):
                         bias=bias[:, first + j, c : c + 1],
                         scale=1.0,
                     )
-                back = psum.tile([P, SLICES, P], F32)
+                back = psum.tile([P, SLICES, P], F32, tag="bank")
                 for c in range(SLICES):
                     nc.tensor.transpose(back[:, c, :], hidden[:, c, :], ident_f32[:])
                 nc.scalar.copy(out=result[:, j, :], in_=back[:].rearrange("r c l -> r (c l)"))
-            nc.scalar.dma_start(out=out[pair].rearrange("s r n -> r s n"), in_=result[:])
+            nc.scalar.dma_start(
+                out=out[group].rearrange("s r n -> r s n"), in_=result[:, 0:count, :]
+            )

@@ -66,6 +66,8 @@ def tile_bnn_pb_kernel(tc, h0, wm1, wv1, bm1, bv1, we1, be1, out):
             sigma_banks.append(bank)
         mean = const.tile([P, N, PACK], BF16)
         nc.vector.tensor_copy(out=mean[:], in_=mean_rows[:].rearrange("p t n -> p n t"))
+        mean_f32 = const.tile([P, N, PACK], F32)
+        nc.scalar.copy(out=mean_f32[:], in_=mean_rows[:].rearrange("p t n -> p n t"))
         mean_banks = []
         for n0 in range(0, N, BF16_BANK_N):
             bank = psum_const.tile([P, BF16_BANK_N, PACK], BF16, name="mean_bank%d" % n0)
@@ -125,13 +127,11 @@ def tile_bnn_pb_kernel(tc, h0, wm1, wv1, bm1, bv1, we1, be1, out):
             weights = work.tile([P, GROUP, N, PACK], BF16, align_bytes=64)
 
             if count == GROUP:
-                scaled_g = work.tile([P, N, PACK], F32)
-                nc.gpsimd.tensor_tensor(
-                    out=scaled_g[:], in0=noise_nt[:, GROUP - 1], in1=sigma[:], op=ALU.mult
-                )
-                nc.gpsimd.tensor_tensor(
-                    out=weights[:, GROUP - 1], in0=scaled_g[:], in1=mean[:], op=ALU.add
-                )
+                sample_g = work.tile([P, N, PACK], F32)
+                nc.scalar.copy(out=sample_g[:], in_=noise_nt[:, GROUP - 1])
+                nc.gpsimd.tensor_tensor(out=sample_g[:], in0=sample_g[:], in1=sigma[:], op=ALU.mult)
+                nc.gpsimd.tensor_tensor(out=sample_g[:], in0=sample_g[:], in1=mean_f32[:], op=ALU.add)
+                nc.scalar.copy(out=weights[:, GROUP - 1], in_=sample_g[:])
 
             scaled_v = work.tile([P, GROUP - 1, N, PACK], F32)
             for i, bank in enumerate(sigma_banks):

@@ -18,7 +18,10 @@ N = 512
 P = 128
 PACK = 4
 SLICES = N // P
-GROUP = 3
+PAIR = 2
+PAIRS = SAMPLES // PAIR
+G_COLS = 128
+V_COLS = N - G_COLS
 F32_BANK_N = 512 // PACK
 BF16_BANK_N = 1024 // PACK
 
@@ -28,13 +31,13 @@ FLOPS = 2 * SAMPLES * ROWS * K * N
 def tile_bnn_pb_kernel(tc, h0, wm1, wv1, bm1, bv1, we1, be1, out):
     nc = tc.nc
     with ExitStack() as ctx:
+        ctx.enter_context(tc.manual_schedule())
         const = ctx.enter_context(tc.tile_pool(name="const", bufs=1))
         loads = ctx.enter_context(tc.tile_pool(name="loads", bufs=3))
         work = ctx.enter_context(tc.tile_pool(name="work", bufs=2))
         packed = ctx.enter_context(tc.tile_pool(name="packed", bufs=3))
-        results = ctx.enter_context(tc.tile_pool(name="results", bufs=3))
-        psum_const = ctx.enter_context(tc.psum_pool(name="psum_const", bufs=1))
-        psum = ctx.enter_context(tc.psum_pool(name="psum", bufs=2))
+        results = ctx.enter_context(tc.tile_pool(name="results", bufs=2))
+        psum = ctx.enter_context(tc.psum_pool(name="psum", bufs=1))
 
         ident_f32 = const.tile([P, P], F32)
         make_identity(nc, ident_f32[:])
@@ -46,7 +49,6 @@ def tile_bnn_pb_kernel(tc, h0, wm1, wv1, bm1, bv1, we1, be1, out):
         mean_rows = const.tile([P, PACK, N], BF16)
         nc.sync.dma_start(out=mean_rows[:], in_=wm1.rearrange("(p t) n -> p t n", t=PACK))
         sigma = const.tile([P, N, PACK], F32)
-        sigma_banks = []
         for n0 in range(0, N, F32_BANK_N):
             cols = slice(n0, n0 + F32_BANK_N)
             nc.scalar.activation(
@@ -55,22 +57,23 @@ def tile_bnn_pb_kernel(tc, h0, wm1, wv1, bm1, bv1, we1, be1, out):
                 func=ACT.Exp,
                 scale=0.5,
             )
-            bank = psum_const.tile([P, F32_BANK_N, PACK], F32, name="sigma_bank%d" % n0)
+        mean = const.tile([P, N, PACK], BF16)
+        nc.vector.tensor_copy(out=mean[:], in_=mean_rows[:].rearrange("p t n -> p n t"))
+
+        sigma_banks = []
+        for n0 in range(0, V_COLS, F32_BANK_N):
+            bank = psum.tile([P, F32_BANK_N, PACK], F32, name="sigma_bank%d" % n0)
             nc.tensor.matmul(
                 out=bank[:].rearrange("p n t -> p (n t)"),
                 lhsT=ident_f32[:],
-                rhs=sigma[:, cols, :].rearrange("p n t -> p (n t)"),
+                rhs=sigma[:, n0 : n0 + F32_BANK_N, :].rearrange("p n t -> p (n t)"),
                 start=True,
                 stop=True,
             )
             sigma_banks.append(bank)
-        mean = const.tile([P, N, PACK], BF16)
-        nc.vector.tensor_copy(out=mean[:], in_=mean_rows[:].rearrange("p t n -> p n t"))
-        mean_f32 = const.tile([P, N, PACK], F32)
-        nc.scalar.copy(out=mean_f32[:], in_=mean_rows[:].rearrange("p t n -> p n t"))
         mean_banks = []
-        for n0 in range(0, N, BF16_BANK_N):
-            bank = psum_const.tile([P, BF16_BANK_N, PACK], BF16, name="mean_bank%d" % n0)
+        for n0 in range(0, V_COLS, BF16_BANK_N):
+            bank = psum.tile([P, BF16_BANK_N, PACK], BF16, name="mean_bank%d" % n0)
             for half in range(0, BF16_BANK_N, F32_BANK_N):
                 nc.tensor.matmul(
                     out=bank[:, half : half + F32_BANK_N, :].rearrange("p n t -> p (n t)"),
@@ -89,9 +92,9 @@ def tile_bnn_pb_kernel(tc, h0, wm1, wv1, bm1, bv1, we1, be1, out):
         nc.sync.dma_start(
             out=bias_stat_rows[SLICES : 2 * SLICES, :], in_=bm1.rearrange("(c l) -> c l", l=P)
         )
-        bias_noise = psum.tile([P, P], BF16, tag="bank")
+        bias_noise = psum.tile([P, P], BF16, tag="product")
         nc.tensor.transpose(bias_noise[:], bias_noise_rows[:], ident_bf16[:])
-        bias_stat = psum.tile([P, P], BF16, tag="bank")
+        bias_stat = psum.tile([P, P], BF16, tag="back")
         nc.tensor.transpose(bias_stat[:], bias_stat_rows[:], ident_bf16[:])
         bias_sigma = const.tile([P, SLICES], F32)
         nc.scalar.activation(out=bias_sigma[:], in_=bias_stat[:, 0:SLICES], func=ACT.Exp, scale=0.5)
@@ -112,72 +115,46 @@ def tile_bnn_pb_kernel(tc, h0, wm1, wv1, bm1, bv1, we1, be1, out):
             op=ALU.add,
         )
 
-        for first in range(0, SAMPLES, GROUP):
-            count = min(GROUP, SAMPLES - first)
-            on_vector = min(GROUP - 1, count)
-            group = slice(first, first + count)
+        def samples_of(i):
+            return slice(i * PAIR, (i + 1) * PAIR)
 
-            noise = loads.tile([P, GROUP, PACK, N], BF16)
-            nc.sync.dma_start(
-                out=noise[:, 0:count], in_=we1[group].rearrange("s (p t) n -> p s t n", t=PACK)
-            )
-            acts = loads.tile([P, GROUP, K], BF16)
-            nc.sync.dma_start(out=acts[:, 0:count], in_=h0[group].rearrange("s r k -> r s k"))
-            noise_nt = noise[:].rearrange("p s t n -> p s n t")
-            weights = work.tile([P, GROUP, N, PACK], BF16, align_bytes=64)
-
-            if count == GROUP:
-                sample_g = work.tile([P, N, PACK], F32)
-                nc.scalar.copy(out=sample_g[:], in_=noise_nt[:, GROUP - 1])
-                nc.gpsimd.tensor_tensor(out=sample_g[:], in0=sample_g[:], in1=sigma[:], op=ALU.mult)
-                nc.gpsimd.tensor_tensor(out=sample_g[:], in0=sample_g[:], in1=mean_f32[:], op=ALU.add)
-                nc.scalar.copy(out=weights[:, GROUP - 1], in_=sample_g[:])
-
-            scaled_v = work.tile([P, GROUP - 1, N, PACK], F32)
-            for i, bank in enumerate(sigma_banks):
-                cols = slice(i * F32_BANK_N, (i + 1) * F32_BANK_N)
-                nc.vector.tensor_tensor(
-                    out=scaled_v[:, 0:on_vector, cols, :],
-                    in0=noise_nt[:, 0:on_vector, cols, :],
-                    in1=bank[:].unsqueeze(1).to_broadcast([P, on_vector, F32_BANK_N, PACK]),
-                    op=ALU.mult,
-                )
-            for i, bank in enumerate(mean_banks):
-                cols = slice(i * BF16_BANK_N, (i + 1) * BF16_BANK_N)
-                nc.vector.tensor_tensor(
-                    out=weights[:, 0:on_vector, cols, :],
-                    in0=scaled_v[:, 0:on_vector, cols, :],
-                    in1=bank[:].unsqueeze(1).to_broadcast([P, on_vector, BF16_BANK_N, PACK]),
-                    op=ALU.add,
-                )
-
+        def quantise_activations(i):
+            acts = loads.tile([P, PAIR, K], BF16)
+            nc.sync.dma_start(out=acts[:], in_=h0[samples_of(i)].rearrange("s r k -> r s k"))
             act_words = acts[:].bitcast(F32).rearrange("r s (q u) -> r s u q", u=2)
-            h_codes = packed.tile([P, GROUP, ROWS], U32, align_bytes=64)
-            h_scales = packed.tile([P, GROUP, ROWS], U8, align_bytes=64)
-            for j in range(count):
-                turned = psum.tile([P, 2, ROWS], F32, tag="bank")
+            turned = psum.tile([P, PAIR, 2, ROWS], F32)
+            for j in range(PAIR):
                 for u in range(2):
-                    nc.tensor.transpose(turned[:, u, :], act_words[:, j, u, :], ident_f32[:])
-                grouped = work.tile([P, ROWS, PACK], BF16, align_bytes=64)
-                nc.scalar.copy(out=grouped[:].bitcast(F32), in_=turned[:].rearrange("q u r -> q r u"))
-                nc.vector.quantize_mx(
-                    out=h_codes[:, j, :].bitcast(FP8X4),
-                    scales=h_scales[:, j, :],
-                    in_=grouped[:].rearrange("q r t -> q (r t)"),
-                )
+                    nc.tensor.transpose(turned[:, j, u, :], act_words[:, j, u, :], ident_f32[:])
+            grouped = work.tile([P, PAIR, ROWS, PACK], BF16, align_bytes=64)
+            nc.scalar.copy(
+                out=grouped[:].bitcast(F32), in_=turned[:].rearrange("q s u r -> q s r u")
+            )
+            h_codes = packed.tile([P, PAIR, ROWS], U32, align_bytes=64)
+            h_scales = packed.tile([P, PAIR, ROWS], U8, align_bytes=64)
+            nc.vector.quantize_mx(
+                out=h_codes[:].rearrange("q s r -> q (s r)").bitcast(FP8X4),
+                scales=h_scales[:].rearrange("q s r -> q (s r)"),
+                in_=grouped[:].rearrange("q s r t -> q (s r t)"),
+            )
+            return h_codes, h_scales
 
-            w_codes = packed.tile([P, GROUP, N], U32, align_bytes=64)
-            w_scales = packed.tile([P, GROUP, N], U8, align_bytes=64)
-            for j in range(count):
-                nc.vector.quantize_mx(
-                    out=w_codes[:, j, :].bitcast(FP8X4),
-                    scales=w_scales[:, j, :],
-                    in_=weights[:, j].rearrange("p n t -> p (n t)"),
-                )
+        def quantise_weights(weights):
+            w_codes = packed.tile([P, PAIR, N], U32, align_bytes=64)
+            w_scales = packed.tile([P, PAIR, N], U8, align_bytes=64)
+            nc.vector.quantize_mx(
+                out=w_codes[:].rearrange("p s n -> p (s n)").bitcast(FP8X4),
+                scales=w_scales[:].rearrange("p s n -> p (s n)"),
+                in_=weights[:].rearrange("p s n t -> p (s n t)"),
+            )
+            return w_codes, w_scales
 
-            result = results.tile([P, GROUP, N], F32)
-            for j in range(count):
-                product = psum.tile([P, SLICES, ROWS], F32, tag="bank")
+        def layer(i, w_packed, h_packed):
+            w_codes, w_scales = w_packed
+            h_codes, h_scales = h_packed
+            result = results.tile([P, PAIR, N], F32)
+            for j in range(PAIR):
+                product = psum.tile([P, SLICES, ROWS], F32)
                 for c in range(SLICES):
                     cols = slice(c * P, (c + 1) * P)
                     nc.tensor.matmul_mx(
@@ -195,13 +172,67 @@ def tile_bnn_pb_kernel(tc, h0, wm1, wv1, bm1, bv1, we1, be1, out):
                         out=hidden[:, c, :],
                         in_=product[:, c, :],
                         func=ACT.Relu,
-                        bias=bias[:, first + j, c : c + 1],
+                        bias=bias[:, i * PAIR + j, c : c + 1],
                         scale=1.0,
                     )
-                back = psum.tile([P, SLICES, P], F32, tag="bank")
+                back = psum.tile([P, SLICES, P], F32)
                 for c in range(SLICES):
                     nc.tensor.transpose(back[:, c, :], hidden[:, c, :], ident_f32[:])
                 nc.scalar.copy(out=result[:, j, :], in_=back[:].rearrange("r c l -> r (c l)"))
-            nc.scalar.dma_start(
-                out=out[group].rearrange("s r n -> r s n"), in_=result[:, 0:count, :]
+            nc.scalar.dma_start(out=out[samples_of(i)].rearrange("s r n -> r s n"), in_=result[:])
+
+        def over_pair(operand, width):
+            return operand.unsqueeze(1).to_broadcast([P, PAIR, width, PACK])
+
+        g_cols = slice(V_COLS, N)
+        h_packed = {0: quantise_activations(0)}
+        weights_before = None
+        for i in range(PAIRS):
+            noise = loads.tile([P, PAIR, PACK, N], BF16)
+            nc.sync.dma_start(
+                out=noise[:], in_=we1[samples_of(i)].rearrange("s (p t) n -> p s t n", t=PACK)
             )
+            noise_nt = noise[:].rearrange("p s t n -> p s n t")
+            weights = packed.tile([P, PAIR, N, PACK], BF16, align_bytes=64)
+
+            scaled_g = work.tile([P, PAIR, G_COLS, PACK], F32)
+            nc.gpsimd.tensor_tensor(
+                out=scaled_g[:],
+                in0=noise_nt[:, :, g_cols, :],
+                in1=over_pair(sigma[:, g_cols, :], G_COLS),
+                op=ALU.mult,
+            )
+            nc.gpsimd.tensor_tensor(
+                out=weights[:, :, g_cols, :],
+                in0=scaled_g[:],
+                in1=over_pair(mean[:, g_cols, :], G_COLS),
+                op=ALU.add,
+            )
+
+            scaled_v = work.tile([P, PAIR, V_COLS, PACK], F32)
+            for b, bank in enumerate(sigma_banks):
+                width = min(F32_BANK_N, V_COLS - b * F32_BANK_N)
+                cols = slice(b * F32_BANK_N, b * F32_BANK_N + width)
+                nc.vector.tensor_tensor(
+                    out=scaled_v[:, :, cols, :],
+                    in0=noise_nt[:, :, cols, :],
+                    in1=over_pair(bank[:, 0:width, :], width),
+                    op=ALU.mult,
+                )
+            if i > 0:
+                w_packed = quantise_weights(weights_before)
+            for b, bank in enumerate(mean_banks):
+                width = min(BF16_BANK_N, V_COLS - b * BF16_BANK_N)
+                cols = slice(b * BF16_BANK_N, b * BF16_BANK_N + width)
+                nc.vector.tensor_tensor(
+                    out=weights[:, :, cols, :],
+                    in0=scaled_v[:, :, cols, :],
+                    in1=over_pair(bank[:, 0:width, :], width),
+                    op=ALU.add,
+                )
+            if i + 1 < PAIRS:
+                h_packed[i + 1] = quantise_activations(i + 1)
+            if i > 0:
+                layer(i - 1, w_packed, h_packed[i - 1])
+            weights_before = weights
+        layer(PAIRS - 1, quantise_weights(weights_before), h_packed[PAIRS - 1])

@@ -37,7 +37,8 @@ def tile_bnn_pb_kernel(tc, h0, wm1, wv1, bm1, bv1, we1, be1, out):
         work = ctx.enter_context(tc.tile_pool(name="work", bufs=2))
         packed = ctx.enter_context(tc.tile_pool(name="packed", bufs=3))
         results = ctx.enter_context(tc.tile_pool(name="results", bufs=2))
-        psum = ctx.enter_context(tc.psum_pool(name="psum", bufs=1))
+        psum_const = ctx.enter_context(tc.psum_pool(name="psum_const", bufs=1))
+        psum = ctx.enter_context(tc.psum_pool(name="psum", bufs=3))
 
         ident_f32 = const.tile([P, P], F32)
         make_identity(nc, ident_f32[:])
@@ -62,7 +63,7 @@ def tile_bnn_pb_kernel(tc, h0, wm1, wv1, bm1, bv1, we1, be1, out):
 
         sigma_banks = []
         for n0 in range(0, V_COLS, F32_BANK_N):
-            bank = psum.tile([P, F32_BANK_N, PACK], F32, name="sigma_bank%d" % n0)
+            bank = psum_const.tile([P, F32_BANK_N, PACK], F32, name="sigma_bank%d" % n0)
             nc.tensor.matmul(
                 out=bank[:].rearrange("p n t -> p (n t)"),
                 lhsT=ident_f32[:],
@@ -73,7 +74,7 @@ def tile_bnn_pb_kernel(tc, h0, wm1, wv1, bm1, bv1, we1, be1, out):
             sigma_banks.append(bank)
         mean_banks = []
         for n0 in range(0, V_COLS, BF16_BANK_N):
-            bank = psum.tile([P, BF16_BANK_N, PACK], BF16, name="mean_bank%d" % n0)
+            bank = psum_const.tile([P, BF16_BANK_N, PACK], BF16, name="mean_bank%d" % n0)
             for half in range(0, BF16_BANK_N, F32_BANK_N):
                 nc.tensor.matmul(
                     out=bank[:, half : half + F32_BANK_N, :].rearrange("p n t -> p (n t)"),
@@ -92,9 +93,9 @@ def tile_bnn_pb_kernel(tc, h0, wm1, wv1, bm1, bv1, we1, be1, out):
         nc.sync.dma_start(
             out=bias_stat_rows[SLICES : 2 * SLICES, :], in_=bm1.rearrange("(c l) -> c l", l=P)
         )
-        bias_noise = psum.tile([P, P], BF16, tag="product")
+        bias_noise = psum.tile([P, P], BF16, tag="bank")
         nc.tensor.transpose(bias_noise[:], bias_noise_rows[:], ident_bf16[:])
-        bias_stat = psum.tile([P, P], BF16, tag="back")
+        bias_stat = psum.tile([P, P], BF16, tag="bank")
         nc.tensor.transpose(bias_stat[:], bias_stat_rows[:], ident_bf16[:])
         bias_sigma = const.tile([P, SLICES], F32)
         nc.scalar.activation(out=bias_sigma[:], in_=bias_stat[:, 0:SLICES], func=ACT.Exp, scale=0.5)
@@ -122,7 +123,7 @@ def tile_bnn_pb_kernel(tc, h0, wm1, wv1, bm1, bv1, we1, be1, out):
             acts = loads.tile([P, PAIR, K], BF16)
             nc.sync.dma_start(out=acts[:], in_=h0[samples_of(i)].rearrange("s r k -> r s k"))
             act_words = acts[:].bitcast(F32).rearrange("r s (q u) -> r s u q", u=2)
-            turned = psum.tile([P, PAIR, 2, ROWS], F32)
+            turned = psum.tile([P, PAIR, 2, ROWS], F32, tag="bank")
             for j in range(PAIR):
                 for u in range(2):
                     nc.tensor.transpose(turned[:, j, u, :], act_words[:, j, u, :], ident_f32[:])
@@ -152,9 +153,9 @@ def tile_bnn_pb_kernel(tc, h0, wm1, wv1, bm1, bv1, we1, be1, out):
         def layer(i, w_packed, h_packed):
             w_codes, w_scales = w_packed
             h_codes, h_scales = h_packed
-            result = results.tile([P, PAIR, N], F32)
+            products = []
             for j in range(PAIR):
-                product = psum.tile([P, SLICES, ROWS], F32)
+                product = psum.tile([P, SLICES, ROWS], F32, tag="bank")
                 for c in range(SLICES):
                     cols = slice(c * P, (c + 1) * P)
                     nc.tensor.matmul_mx(
@@ -166,19 +167,26 @@ def tile_bnn_pb_kernel(tc, h0, wm1, wv1, bm1, bv1, we1, be1, out):
                         start=True,
                         stop=True,
                     )
-                hidden = results.tile([P, SLICES, ROWS], F32)
+                products.append(product)
+            hidden = results.tile([P, PAIR, SLICES, ROWS], F32)
+            for j in range(PAIR):
                 for c in range(SLICES):
                     nc.scalar.activation(
-                        out=hidden[:, c, :],
-                        in_=product[:, c, :],
+                        out=hidden[:, j, c, :],
+                        in_=products[j][:, c, :],
                         func=ACT.Relu,
                         bias=bias[:, i * PAIR + j, c : c + 1],
                         scale=1.0,
                     )
-                back = psum.tile([P, SLICES, P], F32)
+            backs = []
+            for j in range(PAIR):
+                back = psum.tile([P, SLICES, P], F32, tag="bank")
                 for c in range(SLICES):
-                    nc.tensor.transpose(back[:, c, :], hidden[:, c, :], ident_f32[:])
-                nc.scalar.copy(out=result[:, j, :], in_=back[:].rearrange("r c l -> r (c l)"))
+                    nc.tensor.transpose(back[:, c, :], hidden[:, j, c, :], ident_f32[:])
+                backs.append(back)
+            result = results.tile([P, PAIR, N], F32)
+            for j in range(PAIR):
+                nc.scalar.copy(out=result[:, j, :], in_=backs[j][:].rearrange("r c l -> r (c l)"))
             nc.scalar.dma_start(out=out[samples_of(i)].rearrange("s r n -> r s n"), in_=result[:])
 
         def over_pair(operand, width):

@@ -20,7 +20,7 @@ PACK = 4
 SLICES = N // P
 PAIR = 2
 PAIRS = SAMPLES // PAIR
-G_COLS = 128
+G_COLS = 96
 V_COLS = N - G_COLS
 F32_BANK_N = 512 // PACK
 BF16_BANK_N = 1024 // PACK
@@ -38,7 +38,7 @@ def tile_bnn_pb_kernel(tc, h0, wm1, wv1, bm1, bv1, we1, be1, out):
         packed = ctx.enter_context(tc.tile_pool(name="packed", bufs=3))
         results = ctx.enter_context(tc.tile_pool(name="results", bufs=2))
         psum_const = ctx.enter_context(tc.psum_pool(name="psum_const", bufs=1))
-        psum = ctx.enter_context(tc.psum_pool(name="psum", bufs=3))
+        psum = ctx.enter_context(tc.psum_pool(name="psum", bufs=2))
 
         ident_f32 = const.tile([P, P], F32)
         make_identity(nc, ident_f32[:])

@@ -20,7 +20,7 @@ PACK = 4
 SLICES = N // P
 PAIR = 2
 PAIRS = SAMPLES // PAIR
-G_COLS = 96
+G_COLS = 144
 V_COLS = N - G_COLS
 F32_BANK_N = 512 // PACK
 BF16_BANK_N = 1024 // PACK
@@ -33,12 +33,12 @@ def tile_bnn_pb_kernel(tc, h0, wm1, wv1, bm1, bv1, we1, be1, out):
     with ExitStack() as ctx:
         ctx.enter_context(tc.manual_schedule())
         const = ctx.enter_context(tc.tile_pool(name="const", bufs=1))
-        loads = ctx.enter_context(tc.tile_pool(name="loads", bufs=3))
+        loads = ctx.enter_context(tc.tile_pool(name="loads", bufs=4))
         work = ctx.enter_context(tc.tile_pool(name="work", bufs=2))
-        packed = ctx.enter_context(tc.tile_pool(name="packed", bufs=3))
+        packed = ctx.enter_context(tc.tile_pool(name="packed", bufs=4))
         results = ctx.enter_context(tc.tile_pool(name="results", bufs=2))
         psum_const = ctx.enter_context(tc.psum_pool(name="psum_const", bufs=1))
-        psum = ctx.enter_context(tc.psum_pool(name="psum", bufs=2))
+        psum = ctx.enter_context(tc.psum_pool(name="psum", bufs=3))
 
         ident_f32 = const.tile([P, P], F32)
         make_identity(nc, ident_f32[:])
@@ -119,7 +119,7 @@ def tile_bnn_pb_kernel(tc, h0, wm1, wv1, bm1, bv1, we1, be1, out):
         def samples_of(i):
             return slice(i * PAIR, (i + 1) * PAIR)
 
-        def quantise_activations(i):
+        def turn_activations(i):
             acts = loads.tile([P, PAIR, K], BF16)
             nc.sync.dma_start(out=acts[:], in_=h0[samples_of(i)].rearrange("s r k -> r s k"))
             act_words = acts[:].bitcast(F32).rearrange("r s (q u) -> r s u q", u=2)
@@ -131,6 +131,9 @@ def tile_bnn_pb_kernel(tc, h0, wm1, wv1, bm1, bv1, we1, be1, out):
             nc.scalar.copy(
                 out=grouped[:].bitcast(F32), in_=turned[:].rearrange("q s u r -> q s r u")
             )
+            return grouped
+
+        def quantise_activations(grouped):
             h_codes = packed.tile([P, PAIR, ROWS], U32, align_bytes=64)
             h_scales = packed.tile([P, PAIR, ROWS], U8, align_bytes=64)
             nc.vector.quantize_mx(
@@ -193,7 +196,8 @@ def tile_bnn_pb_kernel(tc, h0, wm1, wv1, bm1, bv1, we1, be1, out):
             return operand.unsqueeze(1).to_broadcast([P, PAIR, width, PACK])
 
         g_cols = slice(V_COLS, N)
-        h_packed = {0: quantise_activations(0)}
+        h_grouped = {0: turn_activations(0), 1: turn_activations(1)}
+        h_packed = {0: quantise_activations(h_grouped[0])}
         weights_before = None
         for i in range(PAIRS):
             noise = loads.tile([P, PAIR, PACK, N], BF16)
@@ -201,7 +205,7 @@ def tile_bnn_pb_kernel(tc, h0, wm1, wv1, bm1, bv1, we1, be1, out):
                 out=noise[:], in_=we1[samples_of(i)].rearrange("s (p t) n -> p s t n", t=PACK)
             )
             noise_nt = noise[:].rearrange("p s t n -> p s n t")
-            weights = packed.tile([P, PAIR, N, PACK], BF16, align_bytes=64)
+            weights = work.tile([P, PAIR, N, PACK], BF16, align_bytes=64)
 
             scaled_g = work.tile([P, PAIR, G_COLS, PACK], F32)
             nc.gpsimd.tensor_tensor(
@@ -227,6 +231,8 @@ def tile_bnn_pb_kernel(tc, h0, wm1, wv1, bm1, bv1, we1, be1, out):
                     in1=over_pair(bank[:, 0:width, :], width),
                     op=ALU.mult,
                 )
+            if i + 1 < PAIRS:
+                h_packed[i + 1] = quantise_activations(h_grouped[i + 1])
             if i > 0:
                 w_packed = quantise_weights(weights_before)
             for b, bank in enumerate(mean_banks):
@@ -238,8 +244,9 @@ def tile_bnn_pb_kernel(tc, h0, wm1, wv1, bm1, bv1, we1, be1, out):
                     in1=over_pair(bank[:, 0:width, :], width),
                     op=ALU.add,
                 )
-            if i + 1 < PAIRS:
-                h_packed[i + 1] = quantise_activations(i + 1)
+
+            if i + 2 < PAIRS:
+                h_grouped[i + 2] = turn_activations(i + 2)
             if i > 0:
                 layer(i - 1, w_packed, h_packed[i - 1])
             weights_before = weights

@@ -21,7 +21,8 @@ SLICES = N // P
 PAIR = 2
 PAIRS = SAMPLES // PAIR
 G_COLS = 144
-V_COLS = N - G_COLS
+R_COLS = 128
+V_COLS = N - G_COLS - R_COLS
 F32_BANK_N = 512 // PACK
 BF16_BANK_N = 1024 // PACK
 
@@ -39,6 +40,7 @@ def tile_bnn_pb_kernel(tc, h0, wm1, wv1, bm1, bv1, we1, be1, out):
         results = ctx.enter_context(tc.tile_pool(name="results", bufs=2))
         psum_const = ctx.enter_context(tc.psum_pool(name="psum_const", bufs=1))
         psum = ctx.enter_context(tc.psum_pool(name="psum", bufs=3))
+        psum_turn = ctx.enter_context(tc.psum_pool(name="psum_turn", bufs=2))
 
         ident_f32 = const.tile([P, P], F32)
         make_identity(nc, ident_f32[:])
@@ -60,6 +62,18 @@ def tile_bnn_pb_kernel(tc, h0, wm1, wv1, bm1, bv1, we1, be1, out):
             )
         mean = const.tile([P, N, PACK], BF16)
         nc.vector.tensor_copy(out=mean[:], in_=mean_rows[:].rearrange("p t n -> p n t"))
+
+        r_cols = slice(V_COLS, V_COLS + R_COLS)
+        logvar_turned = psum.tile([P, PACK, P], BF16, tag="bank")
+        for t in range(PACK):
+            nc.tensor.transpose(logvar_turned[:, t, :], logvar_rows[:, t, r_cols], ident_bf16[:])
+        sigma_turned = const.tile([P, PACK, P], F32)
+        nc.scalar.activation(out=sigma_turned[:], in_=logvar_turned[:], func=ACT.Exp, scale=0.5)
+        mean_turned_bf16 = psum.tile([P, PACK, P], BF16, tag="bank")
+        for t in range(PACK):
+            nc.tensor.transpose(mean_turned_bf16[:, t, :], mean_rows[:, t, r_cols], ident_bf16[:])
+        mean_turned = const.tile([P, PACK, P], F32)
+        nc.scalar.copy(out=mean_turned[:], in_=mean_turned_bf16[:])
 
         sigma_banks = []
         for n0 in range(0, V_COLS, F32_BANK_N):
@@ -195,15 +209,53 @@ def tile_bnn_pb_kernel(tc, h0, wm1, wv1, bm1, bv1, we1, be1, out):
         def over_pair(operand, width):
             return operand.unsqueeze(1).to_broadcast([P, PAIR, width, PACK])
 
-        g_cols = slice(V_COLS, N)
-        h_grouped = {0: turn_activations(0), 1: turn_activations(1)}
-        h_packed = {0: quantise_activations(h_grouped[0])}
-        weights_before = None
-        for i in range(PAIRS):
+        g_cols = slice(N - G_COLS, N)
+
+        def load_noise(i):
             noise = loads.tile([P, PAIR, PACK, N], BF16)
             nc.sync.dma_start(
                 out=noise[:], in_=we1[samples_of(i)].rearrange("s (p t) n -> p s t n", t=PACK)
             )
+            return noise
+
+        def turn_noise(noise):
+            noise_turned = psum_turn.tile([P, PAIR, PACK, P], BF16, tag="turn")
+            for j in range(PAIR):
+                for t in range(PACK):
+                    nc.tensor.transpose(noise_turned[:, j, t, :], noise[:, j, t, r_cols], ident_bf16[:])
+            return noise_turned
+
+        def add_means_turning_back(scaled_turned, weights):
+            for j in range(PAIR):
+                summed = psum_turn.tile([P, PACK, P], F32, tag="turn")
+                for t in range(PACK):
+                    nc.tensor.matmul(
+                        out=summed[:, t, :],
+                        lhsT=mean_turned[:, t, :],
+                        rhs=ident_f32[:],
+                        is_transpose=True,
+                        start=True,
+                        stop=False,
+                    )
+                    nc.tensor.matmul(
+                        out=summed[:, t, :],
+                        lhsT=scaled_turned[:, j, t, :],
+                        rhs=ident_f32[:],
+                        is_transpose=True,
+                        start=False,
+                        stop=True,
+                    )
+                nc.scalar.copy(
+                    out=weights[:, j, r_cols, :], in_=summed[:].rearrange("p t n -> p n t")
+                )
+
+        h_grouped = {0: turn_activations(0), 1: turn_activations(1)}
+        h_packed = {0: quantise_activations(h_grouped[0])}
+        weights_before = None
+        noise = load_noise(0)
+        noise_turned = turn_noise(noise)
+        for i in range(PAIRS):
+            noise_next = load_noise(i + 1) if i + 1 < PAIRS else None
             noise_nt = noise[:].rearrange("p s t n -> p s n t")
             weights = work.tile([P, PAIR, N, PACK], BF16, align_bytes=64)
 
@@ -220,6 +272,15 @@ def tile_bnn_pb_kernel(tc, h0, wm1, wv1, bm1, bv1, we1, be1, out):
                 in1=over_pair(mean[:, g_cols, :], G_COLS),
                 op=ALU.add,
             )
+
+            scaled_turned = work.tile([P, PAIR, PACK, P], F32)
+            nc.vector.tensor_tensor(
+                out=scaled_turned[:],
+                in0=noise_turned[:],
+                in1=sigma_turned[:].unsqueeze(1).to_broadcast([P, PAIR, PACK, P]),
+                op=ALU.mult,
+            )
+            add_means_turning_back(scaled_turned, weights)
 
             scaled_v = work.tile([P, PAIR, V_COLS, PACK], F32)
             for b, bank in enumerate(sigma_banks):
@@ -245,9 +306,12 @@ def tile_bnn_pb_kernel(tc, h0, wm1, wv1, bm1, bv1, we1, be1, out):
                     op=ALU.add,
                 )
 
+            if i + 1 < PAIRS:
+                noise_turned = turn_noise(noise_next)
             if i + 2 < PAIRS:
                 h_grouped[i + 2] = turn_activations(i + 2)
             if i > 0:
                 layer(i - 1, w_packed, h_packed[i - 1])
             weights_before = weights
+            noise = noise_next
         layer(PAIRS - 1, quantise_weights(weights_before), h_packed[PAIRS - 1])

@@ -20,7 +20,7 @@ PACK = 4
 SLICES = N // P
 PAIR = 2
 PAIRS = SAMPLES // PAIR
-G_COLS = 144
+G_COLS = 128
 R_COLS = 128
 V_COLS = N - G_COLS - R_COLS
 F32_BANK_N = 512 // PACK

@@ -23,6 +23,8 @@ PAIRS = SAMPLES // PAIR
 G_COLS = 128
 R_COLS = 128
 V_COLS = N - G_COLS - R_COLS
+H_BATCHES = ((0, 2), (2, 2), (4, 4), (8, 4), (12, 4))
+H_AHEAD = 3
 F32_BANK_N = 512 // PACK
 BF16_BANK_N = 1024 // PACK
 
@@ -133,7 +135,15 @@ def tile_bnn_pb_kernel(tc, h0, wm1, wv1, bm1, bv1, we1, be1, out):
         def samples_of(i):
             return slice(i * PAIR, (i + 1) * PAIR)
 
+        batch_of = {}
+        for first, pairs in H_BATCHES:
+            for i in range(first, first + pairs):
+                batch_of[i] = (first, pairs)
+        h_grouped = {}
+        h_packed = {}
+
         def turn_activations(i):
+            first, pairs = batch_of[i]
             acts = loads.tile([P, PAIR, K], BF16)
             nc.sync.dma_start(out=acts[:], in_=h0[samples_of(i)].rearrange("s r k -> r s k"))
             act_words = acts[:].bitcast(F32).rearrange("r s (q u) -> r s u q", u=2)
@@ -141,21 +151,24 @@ def tile_bnn_pb_kernel(tc, h0, wm1, wv1, bm1, bv1, we1, be1, out):
             for j in range(PAIR):
                 for u in range(2):
                     nc.tensor.transpose(turned[:, j, u, :], act_words[:, j, u, :], ident_f32[:])
-            grouped = work.tile([P, PAIR, ROWS, PACK], BF16, align_bytes=64)
+            if i == first:
+                grouped = work.tile([P, pairs * PAIR, ROWS, PACK], BF16, align_bytes=64)
+                h_grouped[first] = grouped
             nc.scalar.copy(
-                out=grouped[:].bitcast(F32), in_=turned[:].rearrange("q s u r -> q s r u")
+                out=h_grouped[first][:, samples_of(i - first), :, :].bitcast(F32),
+                in_=turned[:].rearrange("q s u r -> q s r u"),
             )
-            return grouped
 
-        def quantise_activations(grouped):
-            h_codes = packed.tile([P, PAIR, ROWS], U32, align_bytes=64)
-            h_scales = packed.tile([P, PAIR, ROWS], U8, align_bytes=64)
+        def quantise_activations(first):
+            pairs = batch_of[first][1]
+            h_codes = packed.tile([P, pairs * PAIR, ROWS], U32, align_bytes=64)
+            h_scales = packed.tile([P, pairs * PAIR, ROWS], U8, align_bytes=64)
             nc.vector.quantize_mx(
                 out=h_codes[:].rearrange("q s r -> q (s r)").bitcast(FP8X4),
                 scales=h_scales[:].rearrange("q s r -> q (s r)"),
-                in_=grouped[:].rearrange("q s r t -> q (s r t)"),
+                in_=h_grouped[first][:].rearrange("q s r t -> q (s r t)"),
             )
-            return h_codes, h_scales
+            h_packed[first] = (h_codes, h_scales)
 
         def quantise_weights(weights):
             w_codes = packed.tile([P, PAIR, N], U32, align_bytes=64)
@@ -167,9 +180,11 @@ def tile_bnn_pb_kernel(tc, h0, wm1, wv1, bm1, bv1, we1, be1, out):
             )
             return w_codes, w_scales
 
-        def layer(i, w_packed, h_packed):
+        def layer(i, w_packed):
             w_codes, w_scales = w_packed
-            h_codes, h_scales = h_packed
+            first = batch_of[i][0]
+            h_codes, h_scales = h_packed[first]
+            h_at = (i - first) * PAIR
             products = []
             for j in range(PAIR):
                 product = psum.tile([P, SLICES, ROWS], F32, tag="bank")
@@ -179,8 +194,8 @@ def tile_bnn_pb_kernel(tc, h0, wm1, wv1, bm1, bv1, we1, be1, out):
                         out=product[:, c, :],
                         lhsT=w_codes[:, j, cols].bitcast(FP8X4),
                         lhsT_scale=w_scales[:, j, cols],
-                        rhs=h_codes[:, j, :].bitcast(FP8X4),
-                        rhs_scale=h_scales[:, j, :],
+                        rhs=h_codes[:, h_at + j, :].bitcast(FP8X4),
+                        rhs_scale=h_scales[:, h_at + j, :],
                         start=True,
                         stop=True,
                     )
@@ -249,8 +264,9 @@ def tile_bnn_pb_kernel(tc, h0, wm1, wv1, bm1, bv1, we1, be1, out):
                     out=weights[:, j, r_cols, :], in_=summed[:].rearrange("p t n -> p n t")
                 )
 
-        h_grouped = {0: turn_activations(0), 1: turn_activations(1)}
-        h_packed = {0: quantise_activations(h_grouped[0])}
+        for i in range(H_AHEAD):
+            turn_activations(i)
+        quantise_activations(0)
         weights_before = None
         noise = load_noise(0)
         noise_turned = turn_noise(noise)
@@ -292,8 +308,8 @@ def tile_bnn_pb_kernel(tc, h0, wm1, wv1, bm1, bv1, we1, be1, out):
                     in1=over_pair(bank[:, 0:width, :], width),
                     op=ALU.mult,
                 )
-            if i + 1 < PAIRS:
-                h_packed[i + 1] = quantise_activations(h_grouped[i + 1])
+            if i > 0 and batch_of[i - 1][0] == i - 1 and i > 1:
+                quantise_activations(i - 1)
             if i > 0:
                 w_packed = quantise_weights(weights_before)
             for b, bank in enumerate(mean_banks):
@@ -308,10 +324,10 @@ def tile_bnn_pb_kernel(tc, h0, wm1, wv1, bm1, bv1, we1, be1, out):
 
             if i + 1 < PAIRS:
                 noise_turned = turn_noise(noise_next)
-            if i + 2 < PAIRS:
-                h_grouped[i + 2] = turn_activations(i + 2)
+            if i + H_AHEAD < PAIRS:
+                turn_activations(i + H_AHEAD)
             if i > 0:
-                layer(i - 1, w_packed, h_packed[i - 1])
+                layer(i - 1, w_packed)
             weights_before = weights
             noise = noise_next
-        layer(PAIRS - 1, quantise_weights(weights_before), h_packed[PAIRS - 1])
+        layer(PAIRS - 1, quantise_weights(weights_before))

@@ -170,17 +170,20 @@ def tile_bnn_pb_kernel(tc, h0, wm1, wv1, bm1, bv1, we1, be1, out):
             )
             h_packed[first] = (h_codes, h_scales)
 
-        def quantise_weights(weights):
+        def quantise_weights(weights, calls):
             w_codes = packed.tile([P, PAIR, N], U32, align_bytes=64)
             w_scales = packed.tile([P, PAIR, N], U8, align_bytes=64)
-            nc.vector.quantize_mx(
-                out=w_codes[:].rearrange("p s n -> p (s n)").bitcast(FP8X4),
-                scales=w_scales[:].rearrange("p s n -> p (s n)"),
-                in_=weights[:].rearrange("p s n t -> p (s n t)"),
-            )
+            per_call = PAIR // calls
+            for j0 in range(0, PAIR, per_call):
+                part = slice(j0, j0 + per_call)
+                nc.vector.quantize_mx(
+                    out=w_codes[:, part, :].rearrange("p s n -> p (s n)").bitcast(FP8X4),
+                    scales=w_scales[:, part, :].rearrange("p s n -> p (s n)"),
+                    in_=weights[:, part, :, :].rearrange("p s n t -> p (s n t)"),
+                )
             return w_codes, w_scales
 
-        def layer(i, w_packed):
+        def layer(i, w_packed, vector_helps):
             w_codes, w_scales = w_packed
             first = batch_of[i][0]
             h_codes, h_scales = h_packed[first]
@@ -203,13 +206,23 @@ def tile_bnn_pb_kernel(tc, h0, wm1, wv1, bm1, bv1, we1, be1, out):
             hidden = results.tile([P, PAIR, SLICES, ROWS], F32)
             for j in range(PAIR):
                 for c in range(SLICES):
-                    nc.scalar.activation(
-                        out=hidden[:, j, c, :],
-                        in_=products[j][:, c, :],
-                        func=ACT.Relu,
-                        bias=bias[:, i * PAIR + j, c : c + 1],
-                        scale=1.0,
-                    )
+                    if vector_helps and j == PAIR - 1:
+                        nc.vector.tensor_scalar(
+                            out=hidden[:, j, c, :],
+                            in0=products[j][:, c, :],
+                            scalar1=bias[:, i * PAIR + j, c : c + 1],
+                            scalar2=0.0,
+                            op0=ALU.add,
+                            op1=ALU.max,
+                        )
+                    else:
+                        nc.scalar.activation(
+                            out=hidden[:, j, c, :],
+                            in_=products[j][:, c, :],
+                            func=ACT.Relu,
+                            bias=bias[:, i * PAIR + j, c : c + 1],
+                            scale=1.0,
+                        )
             backs = []
             for j in range(PAIR):
                 back = psum.tile([P, SLICES, P], F32, tag="bank")
@@ -218,8 +231,12 @@ def tile_bnn_pb_kernel(tc, h0, wm1, wv1, bm1, bv1, we1, be1, out):
                 backs.append(back)
             result = results.tile([P, PAIR, N], F32)
             for j in range(PAIR):
-                nc.scalar.copy(out=result[:, j, :], in_=backs[j][:].rearrange("r c l -> r (c l)"))
-            nc.scalar.dma_start(out=out[samples_of(i)].rearrange("s r n -> r s n"), in_=result[:])
+                if vector_helps and j == PAIR - 1:
+                    nc.vector.tensor_copy(out=result[:, j, :], in_=backs[j][:].rearrange("r c l -> r (c l)"))
+                    nc.sync.dma_start(out=out[i * PAIR + j], in_=result[:, j, :])
+                else:
+                    nc.scalar.copy(out=result[:, j, :], in_=backs[j][:].rearrange("r c l -> r (c l)"))
+                    nc.scalar.dma_start(out=out[i * PAIR + j], in_=result[:, j, :])
 
         def over_pair(operand, width):
             return operand.unsqueeze(1).to_broadcast([P, PAIR, width, PACK])
@@ -311,7 +328,7 @@ def tile_bnn_pb_kernel(tc, h0, wm1, wv1, bm1, bv1, we1, be1, out):
             if i > 0 and batch_of[i - 1][0] == i - 1 and i > 1:
                 quantise_activations(i - 1)
             if i > 0:
-                w_packed = quantise_weights(weights_before)
+                w_packed = quantise_weights(weights_before, 1)
             for b, bank in enumerate(mean_banks):
                 width = min(BF16_BANK_N, V_COLS - b * BF16_BANK_N)
                 cols = slice(b * BF16_BANK_N, b * BF16_BANK_N + width)
@@ -327,7 +344,7 @@ def tile_bnn_pb_kernel(tc, h0, wm1, wv1, bm1, bv1, we1, be1, out):
             if i + H_AHEAD < PAIRS:
                 turn_activations(i + H_AHEAD)
             if i > 0:
-                layer(i - 1, w_packed)
+                layer(i - 1, w_packed, False)
             weights_before = weights
             noise = noise_next
-        layer(PAIRS - 1, quantise_weights(weights_before))
+        layer(PAIRS - 1, quantise_weights(weights_before, PAIR), True)

@@ -20,10 +20,11 @@ PACK = 4
 SLICES = N // P
 PAIR = 2
 PAIRS = SAMPLES // PAIR
-G_COLS = 128
+G_COLS = 160
 R_COLS = 128
 V_COLS = N - G_COLS - R_COLS
 H_BATCHES = ((0, 2), (2, 2), (4, 4), (8, 4), (12, 4))
+G_AHEAD = 3
 H_AHEAD = 3
 F32_BANK_N = 512 // PACK
 BF16_BANK_N = 1024 // PACK
@@ -244,11 +245,18 @@ def tile_bnn_pb_kernel(tc, h0, wm1, wv1, bm1, bv1, we1, be1, out):
         g_cols = slice(N - G_COLS, N)
 
         def load_noise(i):
-            noise = loads.tile([P, PAIR, PACK, N], BF16)
+            noise = loads.tile([P, PAIR, PACK, N], BF16, bufs=5)
             nc.sync.dma_start(
                 out=noise[:], in_=we1[samples_of(i)].rearrange("s (p t) n -> p s t n", t=PACK)
             )
             return noise
+
+        def regroup_noise(noise):
+            noise_g = work.tile([P, PAIR, G_COLS, PACK], BF16, bufs=4)
+            nc.scalar.copy(
+                out=noise_g[:], in_=noise[:, :, :, g_cols].rearrange("p s t n -> p s n t")
+            )
+            return noise_g
 
         def turn_noise(noise):
             noise_turned = psum_turn.tile([P, PAIR, PACK, P], BF16, tag="turn")
@@ -285,17 +293,22 @@ def tile_bnn_pb_kernel(tc, h0, wm1, wv1, bm1, bv1, we1, be1, out):
             turn_activations(i)
         quantise_activations(0)
         weights_before = None
-        noise = load_noise(0)
-        noise_turned = turn_noise(noise)
+        noises = []
+        noises_g = []
+        for i in range(G_AHEAD):
+            noises.append(load_noise(i))
+        noises_g.append(regroup_noise(noises[0]))
+        noise_turned = turn_noise(noises[0])
         for i in range(PAIRS):
-            noise_next = load_noise(i + 1) if i + 1 < PAIRS else None
-            noise_nt = noise[:].rearrange("p s t n -> p s n t")
+            if i + G_AHEAD < PAIRS:
+                noises.append(load_noise(i + G_AHEAD))
+            noise_nt = noises[i][:].rearrange("p s t n -> p s n t")
             weights = work.tile([P, PAIR, N, PACK], BF16, align_bytes=64)
 
             scaled_g = work.tile([P, PAIR, G_COLS, PACK], F32)
             nc.gpsimd.tensor_tensor(
                 out=scaled_g[:],
-                in0=noise_nt[:, :, g_cols, :],
+                in0=noises_g[i][:],
                 in1=over_pair(sigma[:, g_cols, :], G_COLS),
                 op=ALU.mult,
             )
@@ -314,6 +327,8 @@ def tile_bnn_pb_kernel(tc, h0, wm1, wv1, bm1, bv1, we1, be1, out):
                 op=ALU.mult,
             )
             add_means_turning_back(scaled_turned, weights)
+            for ahead in range(len(noises_g), min(i + G_AHEAD + 1, PAIRS)):
+                noises_g.append(regroup_noise(noises[ahead]))
 
             scaled_v = work.tile([P, PAIR, V_COLS, PACK], F32)
             for b, bank in enumerate(sigma_banks):
@@ -340,11 +355,10 @@ def tile_bnn_pb_kernel(tc, h0, wm1, wv1, bm1, bv1, we1, be1, out):
                 )
 
             if i + 1 < PAIRS:
-                noise_turned = turn_noise(noise_next)
+                noise_turned = turn_noise(noises[i + 1])
             if i + H_AHEAD < PAIRS:
                 turn_activations(i + H_AHEAD)
             if i > 0:
                 layer(i - 1, w_packed, False)
             weights_before = weights
-            noise = noise_next
         layer(PAIRS - 1, quantise_weights(weights_before, PAIR), True)

@@ -20,14 +20,15 @@ PACK = 4
 SLICES = N // P
 PAIR = 2
 PAIRS = SAMPLES // PAIR
-G_COLS = 160
+G_COLS = 144
 R_COLS = 128
 V_COLS = N - G_COLS - R_COLS
 H_BATCHES = ((0, 2), (2, 2), (4, 4), (8, 4), (12, 4))
 G_AHEAD = 3
 H_AHEAD = 3
-F32_BANK_N = 512 // PACK
-BF16_BANK_N = 1024 // PACK
+RUN = 4
+V_RUNS = V_COLS // RUN
+BANK_RUNS = 512 // (PACK * RUN)
 
 FLOPS = 2 * SAMPLES * ROWS * K * N
 
@@ -54,17 +55,32 @@ def tile_bnn_pb_kernel(tc, h0, wm1, wv1, bm1, bv1, we1, be1, out):
         nc.sync.dma_start(out=logvar_rows[:], in_=wv1.rearrange("(p t) n -> p t n", t=PACK))
         mean_rows = const.tile([P, PACK, N], BF16)
         nc.sync.dma_start(out=mean_rows[:], in_=wm1.rearrange("(p t) n -> p t n", t=PACK))
-        sigma = const.tile([P, N, PACK], F32)
-        for n0 in range(0, N, F32_BANK_N):
-            cols = slice(n0, n0 + F32_BANK_N)
+        v_cols = slice(0, V_COLS)
+        g_cols = slice(N - G_COLS, N)
+        sigma_v = const.tile([P, V_RUNS, PACK, RUN], F32)
+        for c0 in range(0, V_RUNS, BANK_RUNS):
+            runs = slice(c0, min(c0 + BANK_RUNS, V_RUNS))
             nc.scalar.activation(
-                out=sigma[:, cols, :],
-                in_=logvar_rows[:, :, cols].rearrange("p t n -> p n t"),
+                out=sigma_v[:, runs, :, :],
+                in_=logvar_rows[:, :, runs.start * RUN : runs.stop * RUN].rearrange(
+                    "p t (c i) -> p c t i", i=RUN
+                ),
                 func=ACT.Exp,
                 scale=0.5,
             )
-        mean = const.tile([P, N, PACK], BF16)
-        nc.vector.tensor_copy(out=mean[:], in_=mean_rows[:].rearrange("p t n -> p n t"))
+        sigma_g = const.tile([P, G_COLS, PACK], F32)
+        nc.scalar.activation(
+            out=sigma_g[:],
+            in_=logvar_rows[:, :, g_cols].rearrange("p t n -> p n t"),
+            func=ACT.Exp,
+            scale=0.5,
+        )
+        mean_v = const.tile([P, V_RUNS, PACK, RUN], BF16)
+        nc.vector.tensor_copy(
+            out=mean_v[:], in_=mean_rows[:, :, v_cols].rearrange("p t (c i) -> p c t i", i=RUN)
+        )
+        mean_g = const.tile([P, G_COLS, PACK], BF16)
+        nc.vector.tensor_copy(out=mean_g[:], in_=mean_rows[:, :, g_cols].rearrange("p t n -> p n t"))
 
         r_cols = slice(V_COLS, V_COLS + R_COLS)
         logvar_turned = psum.tile([P, PACK, P], BF16, tag="bank")
@@ -79,28 +95,27 @@ def tile_bnn_pb_kernel(tc, h0, wm1, wv1, bm1, bv1, we1, be1, out):
         nc.scalar.copy(out=mean_turned[:], in_=mean_turned_bf16[:])
 
         sigma_banks = []
-        for n0 in range(0, V_COLS, F32_BANK_N):
-            bank = psum_const.tile([P, F32_BANK_N, PACK], F32, name="sigma_bank%d" % n0)
+        for c0 in range(0, V_RUNS, BANK_RUNS):
+            runs = min(BANK_RUNS, V_RUNS - c0)
+            bank = psum_const.tile([P, BANK_RUNS, PACK, RUN], F32, name="sigma_bank%d" % c0)
             nc.tensor.matmul(
-                out=bank[:].rearrange("p n t -> p (n t)"),
+                out=bank[:, 0:runs, :, :].rearrange("p c t i -> p (c t i)"),
                 lhsT=ident_f32[:],
-                rhs=sigma[:, n0 : n0 + F32_BANK_N, :].rearrange("p n t -> p (n t)"),
+                rhs=sigma_v[:, c0 : c0 + runs, :, :].rearrange("p c t i -> p (c t i)"),
                 start=True,
                 stop=True,
             )
-            sigma_banks.append(bank)
-        mean_banks = []
-        for n0 in range(0, V_COLS, BF16_BANK_N):
-            bank = psum_const.tile([P, BF16_BANK_N, PACK], BF16, name="mean_bank%d" % n0)
-            for half in range(0, BF16_BANK_N, F32_BANK_N):
-                nc.tensor.matmul(
-                    out=bank[:, half : half + F32_BANK_N, :].rearrange("p n t -> p (n t)"),
-                    lhsT=ident_bf16[:],
-                    rhs=mean[:, n0 + half : n0 + half + F32_BANK_N, :].rearrange("p n t -> p (n t)"),
-                    start=True,
-                    stop=True,
-                )
-            mean_banks.append(bank)
+            sigma_banks.append((c0, runs, bank))
+        mean_bank = psum_const.tile([P, 2 * BANK_RUNS, PACK, RUN], BF16)
+        for c0 in range(0, V_RUNS, BANK_RUNS):
+            runs = min(BANK_RUNS, V_RUNS - c0)
+            nc.tensor.matmul(
+                out=mean_bank[:, c0 : c0 + runs, :, :].rearrange("p c t i -> p (c t i)"),
+                lhsT=ident_bf16[:],
+                rhs=mean_v[:, c0 : c0 + runs, :, :].rearrange("p c t i -> p (c t i)"),
+                start=True,
+                stop=True,
+            )
 
         bias_noise_rows = const.tile([P, P], BF16)
         nc.sync.dma_start(out=bias_noise_rows[:], in_=be1.rearrange("s o (c l) -> (s o c) l", l=P))
@@ -242,8 +257,6 @@ def tile_bnn_pb_kernel(tc, h0, wm1, wv1, bm1, bv1, we1, be1, out):
         def over_pair(operand, width):
             return operand.unsqueeze(1).to_broadcast([P, PAIR, width, PACK])
 
-        g_cols = slice(N - G_COLS, N)
-
         def load_noise(i):
             noise = loads.tile([P, PAIR, PACK, N], BF16, bufs=5)
             nc.sync.dma_start(
@@ -302,20 +315,19 @@ def tile_bnn_pb_kernel(tc, h0, wm1, wv1, bm1, bv1, we1, be1, out):
         for i in range(PAIRS):
             if i + G_AHEAD < PAIRS:
                 noises.append(load_noise(i + G_AHEAD))
-            noise_nt = noises[i][:].rearrange("p s t n -> p s n t")
             weights = work.tile([P, PAIR, N, PACK], BF16, align_bytes=64)
 
             scaled_g = work.tile([P, PAIR, G_COLS, PACK], F32)
             nc.gpsimd.tensor_tensor(
                 out=scaled_g[:],
                 in0=noises_g[i][:],
-                in1=over_pair(sigma[:, g_cols, :], G_COLS),
+                in1=over_pair(sigma_g[:], G_COLS),
                 op=ALU.mult,
             )
             nc.gpsimd.tensor_tensor(
                 out=weights[:, :, g_cols, :],
                 in0=scaled_g[:],
-                in1=over_pair(mean[:, g_cols, :], G_COLS),
+                in1=over_pair(mean_g[:], G_COLS),
                 op=ALU.add,
             )
 
@@ -330,27 +342,26 @@ def tile_bnn_pb_kernel(tc, h0, wm1, wv1, bm1, bv1, we1, be1, out):
             for ahead in range(len(noises_g), min(i + G_AHEAD + 1, PAIRS)):
                 noises_g.append(regroup_noise(noises[ahead]))
 
-            scaled_v = work.tile([P, PAIR, V_COLS, PACK], F32)
-            for b, bank in enumerate(sigma_banks):
-                width = min(F32_BANK_N, V_COLS - b * F32_BANK_N)
-                cols = slice(b * F32_BANK_N, b * F32_BANK_N + width)
-                nc.vector.tensor_tensor(
-                    out=scaled_v[:, :, cols, :],
-                    in0=noise_nt[:, :, cols, :],
-                    in1=over_pair(bank[:, 0:width, :], width),
-                    op=ALU.mult,
-                )
+            scaled_v = work.tile([P, PAIR, V_RUNS, PACK, RUN], F32)
+            for j in range(PAIR):
+                for c0, runs, bank in sigma_banks:
+                    nc.vector.tensor_tensor(
+                        out=scaled_v[:, j, c0 : c0 + runs, :, :],
+                        in0=noises[i][:, j, :, c0 * RUN : (c0 + runs) * RUN].rearrange(
+                            "p t (c i) -> p c t i", i=RUN
+                        ),
+                        in1=bank[:, 0:runs, :, :],
+                        op=ALU.mult,
+                    )
             if i > 0 and batch_of[i - 1][0] == i - 1 and i > 1:
                 quantise_activations(i - 1)
             if i > 0:
                 w_packed = quantise_weights(weights_before, 1)
-            for b, bank in enumerate(mean_banks):
-                width = min(BF16_BANK_N, V_COLS - b * BF16_BANK_N)
-                cols = slice(b * BF16_BANK_N, b * BF16_BANK_N + width)
+            for j in range(PAIR):
                 nc.vector.tensor_tensor(
-                    out=weights[:, :, cols, :],
-                    in0=scaled_v[:, :, cols, :],
-                    in1=over_pair(bank[:, 0:width, :], width),
+                    out=weights[:, j, v_cols, :].rearrange("p (c i) t -> p c t i", i=RUN),
+                    in0=scaled_v[:, j, :, :, :],
+                    in1=mean_bank[:, 0:V_RUNS, :, :],
                     op=ALU.add,
                 )
 

@@ -20,7 +20,7 @@ PACK = 4
 SLICES = N // P
 PAIR = 2
 PAIRS = SAMPLES // PAIR
-G_COLS = 144
+G_COLS = 152
 R_COLS = 128
 V_COLS = N - G_COLS - R_COLS
 H_BATCHES = ((0, 2), (2, 2), (4, 4), (8, 4), (12, 4))
@@ -342,17 +342,16 @@ def tile_bnn_pb_kernel(tc, h0, wm1, wv1, bm1, bv1, we1, be1, out):
             for ahead in range(len(noises_g), min(i + G_AHEAD + 1, PAIRS)):
                 noises_g.append(regroup_noise(noises[ahead]))
 
-            scaled_v = work.tile([P, PAIR, V_RUNS, PACK, RUN], F32)
-            for j in range(PAIR):
-                for c0, runs, bank in sigma_banks:
-                    nc.vector.tensor_tensor(
-                        out=scaled_v[:, j, c0 : c0 + runs, :, :],
-                        in0=noises[i][:, j, :, c0 * RUN : (c0 + runs) * RUN].rearrange(
-                            "p t (c i) -> p c t i", i=RUN
-                        ),
-                        in1=bank[:, 0:runs, :, :],
-                        op=ALU.mult,
-                    )
+            scaled_v = work.tile([P, V_RUNS, PAIR, PACK, RUN], F32)
+            for c0, runs, bank in sigma_banks:
+                nc.vector.tensor_tensor(
+                    out=scaled_v[:, c0 : c0 + runs, :, :, :],
+                    in0=noises[i][:, :, :, c0 * RUN : (c0 + runs) * RUN].rearrange(
+                        "p s t (c i) -> p c s t i", i=RUN
+                    ),
+                    in1=bank[:, 0:runs, :, :].unsqueeze(2).to_broadcast([P, runs, PAIR, PACK, RUN]),
+                    op=ALU.mult,
+                )
             if i > 0 and batch_of[i - 1][0] == i - 1 and i > 1:
                 quantise_activations(i - 1)
             if i > 0:
@@ -360,7 +359,7 @@ def tile_bnn_pb_kernel(tc, h0, wm1, wv1, bm1, bv1, we1, be1, out):
             for j in range(PAIR):
                 nc.vector.tensor_tensor(
                     out=weights[:, j, v_cols, :].rearrange("p (c i) t -> p c t i", i=RUN),
-                    in0=scaled_v[:, j, :, :, :],
+                    in0=scaled_v[:, :, j, :, :],
                     in1=mean_bank[:, 0:V_RUNS, :, :],
                     op=ALU.add,
                 )

@@ -20,12 +20,13 @@ PACK = 4
 SLICES = N // P
 PAIR = 2
 PAIRS = SAMPLES // PAIR
-G_COLS = 152
+G_COLS = 136
 R_COLS = 128
 V_COLS = N - G_COLS - R_COLS
-H_BATCHES = ((0, 2), (2, 2), (4, 4), (8, 4), (12, 4))
-G_AHEAD = 3
-H_AHEAD = 3
+H_BATCHES = ((0, 1), (1, 1), (2, 2), (4, 4), (8, 4), (12, 4))
+N_AHEAD = 3
+G_AHEAD = 2
+H_AHEAD = 4
 RUN = 4
 V_RUNS = V_COLS // RUN
 BANK_RUNS = 512 // (PACK * RUN)
@@ -51,18 +52,64 @@ def tile_bnn_pb_kernel(tc, h0, wm1, wv1, bm1, bv1, we1, be1, out):
         ident_bf16 = const.tile([P, P], BF16)
         make_identity(nc, ident_bf16[:])
 
+        v_cols = slice(0, V_COLS)
+        r_cols = slice(V_COLS, V_COLS + R_COLS)
+        g_cols = slice(V_COLS + R_COLS, N)
+        v_banks = [(c0, min(BANK_RUNS, V_RUNS - c0)) for c0 in range(0, V_RUNS, BANK_RUNS)]
+
+        def samples_of(i):
+            return slice(i * PAIR, (i + 1) * PAIR)
+
+        noises = []
+        activations = []
+
+        def load_noise(i, calls):
+            noise = loads.tile([P, PAIR, PACK, N], BF16, bufs=5)
+            noises.append(noise)
+            return [
+                (noise[:, part, :, :], we1[i * PAIR + part.start : i * PAIR + part.stop])
+                for part in split_pair(calls)
+            ]
+
+        def split_pair(calls):
+            per_call = PAIR // calls
+            return [slice(j, j + per_call) for j in range(0, PAIR, per_call)]
+
+        def start_load(half):
+            to, rows = half
+            nc.sync.dma_start(out=to, in_=rows.rearrange("s (p t) n -> p s t n", t=PACK))
+
+        def load_activations(i):
+            acts = loads.tile([P, PAIR, K], BF16)
+            nc.sync.dma_start(out=acts[:], in_=h0[samples_of(i)].rearrange("s r k -> r s k"))
+            activations.append(acts)
+
+        bias_stat_rows = const.tile([P, P], BF16)
+        nc.vector.memset(bias_stat_rows[:], 0.0)
+
         logvar_rows = const.tile([P, PACK, N], BF16)
         nc.sync.dma_start(out=logvar_rows[:], in_=wv1.rearrange("(p t) n -> p t n", t=PACK))
+        first_halves = load_noise(0, PAIR)
+        start_load(first_halves[0])
+        start_load(first_halves[1])
         mean_rows = const.tile([P, PACK, N], BF16)
         nc.sync.dma_start(out=mean_rows[:], in_=wm1.rearrange("(p t) n -> p t n", t=PACK))
-        v_cols = slice(0, V_COLS)
-        g_cols = slice(N - G_COLS, N)
+        load_activations(0)
+        bias_noise_rows = const.tile([P, P], BF16)
+        nc.sync.dma_start(out=bias_noise_rows[:], in_=be1.rearrange("s o (c l) -> (s o c) l", l=P))
+        nc.sync.dma_start(out=bias_stat_rows[0:SLICES, :], in_=bv1.rearrange("(c l) -> c l", l=P))
+        nc.sync.dma_start(
+            out=bias_stat_rows[SLICES : 2 * SLICES, :], in_=bm1.rearrange("(c l) -> c l", l=P)
+        )
+        for i in range(1, N_AHEAD):
+            start_load(load_noise(i, 1)[0])
+            load_activations(i)
+
         sigma_v = const.tile([P, V_RUNS, PACK, RUN], F32)
-        for c0 in range(0, V_RUNS, BANK_RUNS):
-            runs = slice(c0, min(c0 + BANK_RUNS, V_RUNS))
+        for c0, runs in v_banks:
             nc.scalar.activation(
-                out=sigma_v[:, runs, :, :],
-                in_=logvar_rows[:, :, runs.start * RUN : runs.stop * RUN].rearrange(
+                out=sigma_v[:, c0 : c0 + runs, :, :],
+                in_=logvar_rows[:, :, c0 * RUN : (c0 + runs) * RUN].rearrange(
                     "p t (c i) -> p c t i", i=RUN
                 ),
                 func=ACT.Exp,
@@ -75,28 +122,10 @@ def tile_bnn_pb_kernel(tc, h0, wm1, wv1, bm1, bv1, we1, be1, out):
             func=ACT.Exp,
             scale=0.5,
         )
-        mean_v = const.tile([P, V_RUNS, PACK, RUN], BF16)
-        nc.vector.tensor_copy(
-            out=mean_v[:], in_=mean_rows[:, :, v_cols].rearrange("p t (c i) -> p c t i", i=RUN)
-        )
-        mean_g = const.tile([P, G_COLS, PACK], BF16)
-        nc.vector.tensor_copy(out=mean_g[:], in_=mean_rows[:, :, g_cols].rearrange("p t n -> p n t"))
-
-        r_cols = slice(V_COLS, V_COLS + R_COLS)
-        logvar_turned = psum.tile([P, PACK, P], BF16, tag="bank")
-        for t in range(PACK):
-            nc.tensor.transpose(logvar_turned[:, t, :], logvar_rows[:, t, r_cols], ident_bf16[:])
-        sigma_turned = const.tile([P, PACK, P], F32)
-        nc.scalar.activation(out=sigma_turned[:], in_=logvar_turned[:], func=ACT.Exp, scale=0.5)
-        mean_turned_bf16 = psum.tile([P, PACK, P], BF16, tag="bank")
-        for t in range(PACK):
-            nc.tensor.transpose(mean_turned_bf16[:, t, :], mean_rows[:, t, r_cols], ident_bf16[:])
-        mean_turned = const.tile([P, PACK, P], F32)
-        nc.scalar.copy(out=mean_turned[:], in_=mean_turned_bf16[:])
 
         sigma_banks = []
-        for c0 in range(0, V_RUNS, BANK_RUNS):
-            runs = min(BANK_RUNS, V_RUNS - c0)
+
+        def fill_sigma_bank(c0, runs):
             bank = psum_const.tile([P, BANK_RUNS, PACK, RUN], F32, name="sigma_bank%d" % c0)
             nc.tensor.matmul(
                 out=bank[:, 0:runs, :, :].rearrange("p c t i -> p (c t i)"),
@@ -106,50 +135,6 @@ def tile_bnn_pb_kernel(tc, h0, wm1, wv1, bm1, bv1, we1, be1, out):
                 stop=True,
             )
             sigma_banks.append((c0, runs, bank))
-        mean_bank = psum_const.tile([P, 2 * BANK_RUNS, PACK, RUN], BF16)
-        for c0 in range(0, V_RUNS, BANK_RUNS):
-            runs = min(BANK_RUNS, V_RUNS - c0)
-            nc.tensor.matmul(
-                out=mean_bank[:, c0 : c0 + runs, :, :].rearrange("p c t i -> p (c t i)"),
-                lhsT=ident_bf16[:],
-                rhs=mean_v[:, c0 : c0 + runs, :, :].rearrange("p c t i -> p (c t i)"),
-                start=True,
-                stop=True,
-            )
-
-        bias_noise_rows = const.tile([P, P], BF16)
-        nc.sync.dma_start(out=bias_noise_rows[:], in_=be1.rearrange("s o (c l) -> (s o c) l", l=P))
-        bias_stat_rows = const.tile([P, P], BF16)
-        nc.vector.memset(bias_stat_rows[:], 0.0)
-        nc.sync.dma_start(out=bias_stat_rows[0:SLICES, :], in_=bv1.rearrange("(c l) -> c l", l=P))
-        nc.sync.dma_start(
-            out=bias_stat_rows[SLICES : 2 * SLICES, :], in_=bm1.rearrange("(c l) -> c l", l=P)
-        )
-        bias_noise = psum.tile([P, P], BF16, tag="bank")
-        nc.tensor.transpose(bias_noise[:], bias_noise_rows[:], ident_bf16[:])
-        bias_stat = psum.tile([P, P], BF16, tag="bank")
-        nc.tensor.transpose(bias_stat[:], bias_stat_rows[:], ident_bf16[:])
-        bias_sigma = const.tile([P, SLICES], F32)
-        nc.scalar.activation(out=bias_sigma[:], in_=bias_stat[:, 0:SLICES], func=ACT.Exp, scale=0.5)
-        bias_mean = const.tile([P, SLICES], F32)
-        nc.scalar.copy(out=bias_mean[:], in_=bias_stat[:, SLICES : 2 * SLICES])
-        bias_scaled = const.tile([P, SAMPLES, SLICES], F32)
-        nc.vector.tensor_tensor(
-            out=bias_scaled[:],
-            in0=bias_noise[:].rearrange("l (s c) -> l s c", c=SLICES),
-            in1=bias_sigma[:].unsqueeze(1).to_broadcast([P, SAMPLES, SLICES]),
-            op=ALU.mult,
-        )
-        bias = const.tile([P, SAMPLES, SLICES], F32)
-        nc.vector.tensor_tensor(
-            out=bias[:],
-            in0=bias_scaled[:],
-            in1=bias_mean[:].unsqueeze(1).to_broadcast([P, SAMPLES, SLICES]),
-            op=ALU.add,
-        )
-
-        def samples_of(i):
-            return slice(i * PAIR, (i + 1) * PAIR)
 
         batch_of = {}
         for first, pairs in H_BATCHES:
@@ -160,15 +145,13 @@ def tile_bnn_pb_kernel(tc, h0, wm1, wv1, bm1, bv1, we1, be1, out):
 
         def turn_activations(i):
             first, pairs = batch_of[i]
-            acts = loads.tile([P, PAIR, K], BF16)
-            nc.sync.dma_start(out=acts[:], in_=h0[samples_of(i)].rearrange("s r k -> r s k"))
-            act_words = acts[:].bitcast(F32).rearrange("r s (q u) -> r s u q", u=2)
+            act_words = activations[i][:].bitcast(F32).rearrange("r s (q u) -> r s u q", u=2)
             turned = psum.tile([P, PAIR, 2, ROWS], F32, tag="bank")
             for j in range(PAIR):
                 for u in range(2):
                     nc.tensor.transpose(turned[:, j, u, :], act_words[:, j, u, :], ident_f32[:])
             if i == first:
-                grouped = work.tile([P, pairs * PAIR, ROWS, PACK], BF16, align_bytes=64)
+                grouped = work.tile([P, pairs * PAIR, ROWS, PACK], BF16, bufs=3, align_bytes=64)
                 h_grouped[first] = grouped
             nc.scalar.copy(
                 out=h_grouped[first][:, samples_of(i - first), :, :].bitcast(F32),
@@ -186,20 +169,20 @@ def tile_bnn_pb_kernel(tc, h0, wm1, wv1, bm1, bv1, we1, be1, out):
             )
             h_packed[first] = (h_codes, h_scales)
 
-        def quantise_weights(weights, calls):
+        def new_packed():
             w_codes = packed.tile([P, PAIR, N], U32, align_bytes=64)
             w_scales = packed.tile([P, PAIR, N], U8, align_bytes=64)
-            per_call = PAIR // calls
-            for j0 in range(0, PAIR, per_call):
-                part = slice(j0, j0 + per_call)
-                nc.vector.quantize_mx(
-                    out=w_codes[:, part, :].rearrange("p s n -> p (s n)").bitcast(FP8X4),
-                    scales=w_scales[:, part, :].rearrange("p s n -> p (s n)"),
-                    in_=weights[:, part, :, :].rearrange("p s n t -> p (s n t)"),
-                )
             return w_codes, w_scales
 
-        def layer(i, w_packed, vector_helps):
+        def quantise_weights(weights, w_packed, part):
+            w_codes, w_scales = w_packed
+            nc.vector.quantize_mx(
+                out=w_codes[:, part, :].rearrange("p s n -> p (s n)").bitcast(FP8X4),
+                scales=w_scales[:, part, :].rearrange("p s n -> p (s n)"),
+                in_=weights[:, part, :, :].rearrange("p s n t -> p (s n t)"),
+            )
+
+        def layer(i, w_packed, bias, vector_helps):
             w_codes, w_scales = w_packed
             first = batch_of[i][0]
             h_codes, h_scales = h_packed[first]
@@ -239,6 +222,9 @@ def tile_bnn_pb_kernel(tc, h0, wm1, wv1, bm1, bv1, we1, be1, out):
                             bias=bias[:, i * PAIR + j, c : c + 1],
                             scale=1.0,
                         )
+            return hidden
+
+        def turn_back(i, hidden, vector_helps):
             backs = []
             for j in range(PAIR):
                 back = psum.tile([P, SLICES, P], F32, tag="bank")
@@ -252,24 +238,36 @@ def tile_bnn_pb_kernel(tc, h0, wm1, wv1, bm1, bv1, we1, be1, out):
                     nc.sync.dma_start(out=out[i * PAIR + j], in_=result[:, j, :])
                 else:
                     nc.scalar.copy(out=result[:, j, :], in_=backs[j][:].rearrange("r c l -> r (c l)"))
-                    nc.scalar.dma_start(out=out[i * PAIR + j], in_=result[:, j, :])
+                    nc.sync.dma_start(out=out[i * PAIR + j], in_=result[:, j, :])
 
-        def over_pair(operand, width):
-            return operand.unsqueeze(1).to_broadcast([P, PAIR, width, PACK])
-
-        def load_noise(i):
-            noise = loads.tile([P, PAIR, PACK, N], BF16, bufs=5)
-            nc.sync.dma_start(
-                out=noise[:], in_=we1[samples_of(i)].rearrange("s (p t) n -> p s t n", t=PACK)
-            )
-            return noise
-
-        def regroup_noise(noise):
+        def regroup_noise(noise, parts):
             noise_g = work.tile([P, PAIR, G_COLS, PACK], BF16, bufs=4)
-            nc.scalar.copy(
-                out=noise_g[:], in_=noise[:, :, :, g_cols].rearrange("p s t n -> p s n t")
-            )
+            for part in parts:
+                nc.scalar.copy(
+                    out=noise_g[:, part, :, :],
+                    in_=noise[:, part, :, g_cols].rearrange("p s t n -> p s n t"),
+                )
             return noise_g
+
+        def scale_gpsimd(noise_g, parts):
+            scaled_g = work.tile([P, PAIR, G_COLS, PACK], F32)
+            for part in parts:
+                samples = part.stop - part.start
+                nc.gpsimd.tensor_tensor(
+                    out=scaled_g[:, part, :, :],
+                    in0=noise_g[:, part, :, :],
+                    in1=sigma_g[:].unsqueeze(1).to_broadcast([P, samples, G_COLS, PACK]),
+                    op=ALU.mult,
+                )
+            return scaled_g
+
+        def add_means_gpsimd(scaled_g, weights):
+            nc.gpsimd.tensor_tensor(
+                out=weights[:, :, g_cols, :],
+                in0=scaled_g[:],
+                in1=mean_g[:].unsqueeze(1).to_broadcast([P, PAIR, G_COLS, PACK]),
+                op=ALU.add,
+            )
 
         def turn_noise(noise):
             noise_turned = psum_turn.tile([P, PAIR, PACK, P], BF16, tag="turn")
@@ -277,6 +275,16 @@ def tile_bnn_pb_kernel(tc, h0, wm1, wv1, bm1, bv1, we1, be1, out):
                 for t in range(PACK):
                     nc.tensor.transpose(noise_turned[:, j, t, :], noise[:, j, t, r_cols], ident_bf16[:])
             return noise_turned
+
+        def scale_turned(noise_turned):
+            scaled_turned = work.tile([P, PAIR, PACK, P], F32)
+            nc.vector.tensor_tensor(
+                out=scaled_turned[:],
+                in0=noise_turned[:],
+                in1=sigma_turned[:].unsqueeze(1).to_broadcast([P, PAIR, PACK, P]),
+                op=ALU.mult,
+            )
+            return scaled_turned
 
         def add_means_turning_back(scaled_turned, weights):
             for j in range(PAIR):
@@ -302,73 +310,129 @@ def tile_bnn_pb_kernel(tc, h0, wm1, wv1, bm1, bv1, we1, be1, out):
                     out=weights[:, j, r_cols, :], in_=summed[:].rearrange("p t n -> p n t")
                 )
 
-        for i in range(H_AHEAD):
-            turn_activations(i)
-        quantise_activations(0)
-        weights_before = None
-        noises = []
-        noises_g = []
-        for i in range(G_AHEAD):
-            noises.append(load_noise(i))
-        noises_g.append(regroup_noise(noises[0]))
-        noise_turned = turn_noise(noises[0])
-        for i in range(PAIRS):
-            if i + G_AHEAD < PAIRS:
-                noises.append(load_noise(i + G_AHEAD))
-            weights = work.tile([P, PAIR, N, PACK], BF16, align_bytes=64)
-
-            scaled_g = work.tile([P, PAIR, G_COLS, PACK], F32)
-            nc.gpsimd.tensor_tensor(
-                out=scaled_g[:],
-                in0=noises_g[i][:],
-                in1=over_pair(sigma_g[:], G_COLS),
+        def scale(noise, scaled_v, part, c0, runs, sigma):
+            samples = part.stop - part.start
+            nc.vector.tensor_tensor(
+                out=scaled_v[:, c0 : c0 + runs, part, :, :],
+                in0=noise[:, part, :, c0 * RUN : (c0 + runs) * RUN].rearrange(
+                    "p s t (c i) -> p c s t i", i=RUN
+                ),
+                in1=sigma.unsqueeze(2).to_broadcast([P, runs, samples, PACK, RUN]),
                 op=ALU.mult,
             )
-            nc.gpsimd.tensor_tensor(
-                out=weights[:, :, g_cols, :],
-                in0=scaled_g[:],
-                in1=over_pair(mean_g[:], G_COLS),
+
+        def add_means(scaled_v, weights, j):
+            nc.vector.tensor_tensor(
+                out=weights[:, j, v_cols, :].rearrange("p (c i) t -> p c t i", i=RUN),
+                in0=scaled_v[:, :, j, :, :],
+                in1=mean_bank[:, 0:V_RUNS, :, :],
                 op=ALU.add,
             )
 
-            scaled_turned = work.tile([P, PAIR, PACK, P], F32)
+        def make_bias():
+            bias_noise = psum.tile([P, P], BF16, tag="bank")
+            nc.tensor.transpose(bias_noise[:], bias_noise_rows[:], ident_bf16[:])
+            bias_stat = psum.tile([P, P], BF16, tag="bank")
+            nc.tensor.transpose(bias_stat[:], bias_stat_rows[:], ident_bf16[:])
+            bias_sigma = const.tile([P, SLICES], F32)
+            nc.scalar.activation(out=bias_sigma[:], in_=bias_stat[:, 0:SLICES], func=ACT.Exp, scale=0.5)
+            bias_scaled = const.tile([P, SAMPLES, SLICES], F32)
             nc.vector.tensor_tensor(
-                out=scaled_turned[:],
-                in0=noise_turned[:],
-                in1=sigma_turned[:].unsqueeze(1).to_broadcast([P, PAIR, PACK, P]),
+                out=bias_scaled[:],
+                in0=bias_noise[:].rearrange("l (s c) -> l s c", c=SLICES),
+                in1=bias_sigma[:].unsqueeze(1).to_broadcast([P, SAMPLES, SLICES]),
                 op=ALU.mult,
             )
-            add_means_turning_back(scaled_turned, weights)
-            for ahead in range(len(noises_g), min(i + G_AHEAD + 1, PAIRS)):
-                noises_g.append(regroup_noise(noises[ahead]))
+            bias = const.tile([P, SAMPLES, SLICES], F32)
+            nc.vector.tensor_tensor(
+                out=bias[:],
+                in0=bias_scaled[:],
+                in1=bias_stat[:, SLICES : 2 * SLICES].unsqueeze(1).to_broadcast([P, SAMPLES, SLICES]),
+                op=ALU.add,
+            )
+            return bias
 
+        one_by_one = split_pair(PAIR)
+        together = split_pair(1)
+        weights = work.tile([P, PAIR, N, PACK], BF16, bufs=1, align_bytes=64)
+        noises_g = [regroup_noise(noises[0], one_by_one)]
+        logvar_turned = psum.tile([P, PACK, P], BF16, tag="bank")
+        for t in range(PACK):
+            nc.tensor.transpose(logvar_turned[:, t, :], logvar_rows[:, t, r_cols], ident_bf16[:])
+        sigma_turned = const.tile([P, PACK, P], F32)
+        nc.scalar.activation(out=sigma_turned[:], in_=logvar_turned[:], func=ACT.Exp, scale=0.5)
+        mean_g = const.tile([P, G_COLS, PACK], BF16)
+        nc.scalar.copy(out=mean_g[:], in_=mean_rows[:, :, g_cols].rearrange("p t n -> p n t"))
+        add_means_gpsimd(scale_gpsimd(noises_g[0], one_by_one), weights)
+
+        fill_sigma_bank(*v_banks[0])
+        scaled_v = work.tile([P, V_RUNS, PAIR, PACK, RUN], F32)
+        for part in one_by_one:
+            for c0, runs in v_banks:
+                scale(noises[0], scaled_v, part, c0, runs, sigma_v[:, c0 : c0 + runs, :, :])
+        noise_turned = turn_noise(noises[0])
+        mean_bank = psum_const.tile([P, 2 * BANK_RUNS, PACK, RUN], BF16)
+        for c0, runs in v_banks:
+            nc.tensor.matmul(
+                out=mean_bank[:, c0 : c0 + runs, :, :],
+                lhsT=ident_bf16[:],
+                rhs=mean_rows[:, :, c0 * RUN : (c0 + runs) * RUN].rearrange(
+                    "p t (c i) -> p c t i", i=RUN
+                ),
+                start=True,
+                stop=True,
+            )
+        mean_turned_bf16 = psum.tile([P, PACK, P], BF16, tag="bank")
+        for t in range(PACK):
+            nc.tensor.transpose(mean_turned_bf16[:, t, :], mean_rows[:, t, r_cols], ident_bf16[:])
+        mean_turned = const.tile([P, PACK, P], F32)
+        nc.scalar.copy(out=mean_turned[:], in_=mean_turned_bf16[:])
+        fill_sigma_bank(*v_banks[1])
+        add_means_turning_back(scale_turned(noise_turned), weights)
+        for j in range(PAIR):
+            add_means(scaled_v, weights, j)
+        noise_turned = turn_noise(noises[1])
+        noises_g.append(regroup_noise(noises[1], together))
+        turn_activations(0)
+
+        turn_activations(1)
+        noises_g.append(regroup_noise(noises[2], together))
+
+        turned_pairs = 2
+        hidden = None
+        for i in range(1, PAIRS):
+            for ahead in range(len(noises), min(i + N_AHEAD + 1, PAIRS)):
+                start_load(load_noise(ahead, 1)[0])
+            for ahead in range(len(activations), min(i + H_AHEAD + 1, PAIRS)):
+                load_activations(ahead)
+            scaled_g = scale_gpsimd(noises_g[i], together)
             scaled_v = work.tile([P, V_RUNS, PAIR, PACK, RUN], F32)
             for c0, runs, bank in sigma_banks:
-                nc.vector.tensor_tensor(
-                    out=scaled_v[:, c0 : c0 + runs, :, :, :],
-                    in0=noises[i][:, :, :, c0 * RUN : (c0 + runs) * RUN].rearrange(
-                        "p s t (c i) -> p c s t i", i=RUN
-                    ),
-                    in1=bank[:, 0:runs, :, :].unsqueeze(2).to_broadcast([P, runs, PAIR, PACK, RUN]),
-                    op=ALU.mult,
-                )
-            if i > 0 and batch_of[i - 1][0] == i - 1 and i > 1:
+                scale(noises[i], scaled_v, slice(0, PAIR), c0, runs, bank[:, 0:runs, :, :])
+            if batch_of[i - 1][0] == i - 1:
                 quantise_activations(i - 1)
-            if i > 0:
-                w_packed = quantise_weights(weights_before, 1)
-            for j in range(PAIR):
-                nc.vector.tensor_tensor(
-                    out=weights[:, j, v_cols, :].rearrange("p (c i) t -> p c t i", i=RUN),
-                    in0=scaled_v[:, :, j, :, :],
-                    in1=mean_bank[:, 0:V_RUNS, :, :],
-                    op=ALU.add,
-                )
-
+            w_packed = new_packed()
+            quantise_weights(weights, w_packed, slice(0, PAIR))
+            if i == 1:
+                bias = make_bias()
+            scaled_turned = scale_turned(noise_turned)
+            weights = work.tile([P, PAIR, N, PACK], BF16, bufs=1, align_bytes=64)
+            add_means_gpsimd(scaled_g, weights)
+            if i > 1:
+                turn_back(i - 2, hidden, False)
+            add_means_turning_back(scaled_turned, weights)
+            for ahead in range(len(noises_g), min(i + G_AHEAD + 1, PAIRS)):
+                noises_g.append(regroup_noise(noises[ahead], together))
             if i + 1 < PAIRS:
                 noise_turned = turn_noise(noises[i + 1])
-            if i + H_AHEAD < PAIRS:
-                turn_activations(i + H_AHEAD)
-            if i > 0:
-                layer(i - 1, w_packed, False)
-            weights_before = weights
-        layer(PAIRS - 1, quantise_weights(weights_before, PAIR), True)
+            for ahead in range(turned_pairs, min(i + H_AHEAD + 1, PAIRS)):
+                turn_activations(ahead)
+                turned_pairs = ahead + 1
+            last_packed = new_packed() if i + 1 == PAIRS else None
+            for j in range(PAIR):
+                add_means(scaled_v, weights, j)
+                if i + 1 == PAIRS:
+                    quantise_weights(weights, last_packed, slice(j, j + 1))
+            hidden = layer(i - 1, w_packed, bias, False)
+        turn_back(PAIRS - 2, hidden, False)
+        turn_back(PAIRS - 1, layer(PAIRS - 1, last_packed, bias, True), True)

@@ -20,7 +20,7 @@ PACK = 4
 SLICES = N // P
 PAIR = 2
 PAIRS = SAMPLES // PAIR
-G_COLS = 136
+G_COLS = 128
 R_COLS = 128
 V_COLS = N - G_COLS - R_COLS
 H_BATCHES = ((0, 1), (1, 1), (2, 2), (4, 4), (8, 4), (12, 4))
@@ -94,6 +94,7 @@ def tile_bnn_pb_kernel(tc, h0, wm1, wv1, bm1, bv1, we1, be1, out):
         start_load(first_halves[1])
         mean_rows = const.tile([P, PACK, N], BF16)
         nc.sync.dma_start(out=mean_rows[:], in_=wm1.rearrange("(p t) n -> p t n", t=PACK))
+        start_load(load_noise(1, 1)[0])
         load_activations(0)
         bias_noise_rows = const.tile([P, P], BF16)
         nc.sync.dma_start(out=bias_noise_rows[:], in_=be1.rearrange("s o (c l) -> (s o c) l", l=P))
@@ -101,7 +102,8 @@ def tile_bnn_pb_kernel(tc, h0, wm1, wv1, bm1, bv1, we1, be1, out):
         nc.sync.dma_start(
             out=bias_stat_rows[SLICES : 2 * SLICES, :], in_=bm1.rearrange("(c l) -> c l", l=P)
         )
-        for i in range(1, N_AHEAD):
+        load_activations(1)
+        for i in range(2, N_AHEAD):
             start_load(load_noise(i, 1)[0])
             load_activations(i)
 
@@ -182,14 +184,14 @@ def tile_bnn_pb_kernel(tc, h0, wm1, wv1, bm1, bv1, we1, be1, out):
                 in_=weights[:, part, :, :].rearrange("p s n t -> p (s n t)"),
             )
 
-        def layer(i, w_packed, bias, vector_helps):
+        def layer(i, w_packed, bias, vector_helps, pool, tag):
             w_codes, w_scales = w_packed
             first = batch_of[i][0]
             h_codes, h_scales = h_packed[first]
             h_at = (i - first) * PAIR
             products = []
             for j in range(PAIR):
-                product = psum.tile([P, SLICES, ROWS], F32, tag="bank")
+                product = pool.tile([P, SLICES, ROWS], F32, tag=tag)
                 for c in range(SLICES):
                     cols = slice(c * P, (c + 1) * P)
                     nc.tensor.matmul_mx(
@@ -355,12 +357,12 @@ def tile_bnn_pb_kernel(tc, h0, wm1, wv1, bm1, bv1, we1, be1, out):
         one_by_one = split_pair(PAIR)
         together = split_pair(1)
         weights = work.tile([P, PAIR, N, PACK], BF16, bufs=1, align_bytes=64)
-        noises_g = [regroup_noise(noises[0], one_by_one)]
         logvar_turned = psum.tile([P, PACK, P], BF16, tag="bank")
         for t in range(PACK):
             nc.tensor.transpose(logvar_turned[:, t, :], logvar_rows[:, t, r_cols], ident_bf16[:])
         sigma_turned = const.tile([P, PACK, P], F32)
         nc.scalar.activation(out=sigma_turned[:], in_=logvar_turned[:], func=ACT.Exp, scale=0.5)
+        noises_g = [regroup_noise(noises[0], one_by_one)]
         mean_g = const.tile([P, G_COLS, PACK], BF16)
         nc.scalar.copy(out=mean_g[:], in_=mean_rows[:, :, g_cols].rearrange("p t n -> p n t"))
         add_means_gpsimd(scale_gpsimd(noises_g[0], one_by_one), weights)
@@ -387,12 +389,12 @@ def tile_bnn_pb_kernel(tc, h0, wm1, wv1, bm1, bv1, we1, be1, out):
             nc.tensor.transpose(mean_turned_bf16[:, t, :], mean_rows[:, t, r_cols], ident_bf16[:])
         mean_turned = const.tile([P, PACK, P], F32)
         nc.scalar.copy(out=mean_turned[:], in_=mean_turned_bf16[:])
+        noises_g.append(regroup_noise(noises[1], together))
         fill_sigma_bank(*v_banks[1])
         add_means_turning_back(scale_turned(noise_turned), weights)
         for j in range(PAIR):
             add_means(scaled_v, weights, j)
         noise_turned = turn_noise(noises[1])
-        noises_g.append(regroup_noise(noises[1], together))
         turn_activations(0)
 
         turn_activations(1)
@@ -409,17 +411,23 @@ def tile_bnn_pb_kernel(tc, h0, wm1, wv1, bm1, bv1, we1, be1, out):
             scaled_v = work.tile([P, V_RUNS, PAIR, PACK, RUN], F32)
             for c0, runs, bank in sigma_banks:
                 scale(noises[i], scaled_v, slice(0, PAIR), c0, runs, bank[:, 0:runs, :, :])
+            last = i + 1 == PAIRS
+            if i == 1:
+                scaled_turned = scale_turned(noise_turned)
             if batch_of[i - 1][0] == i - 1:
                 quantise_activations(i - 1)
             w_packed = new_packed()
             quantise_weights(weights, w_packed, slice(0, PAIR))
             if i == 1:
                 bias = make_bias()
-            scaled_turned = scale_turned(noise_turned)
+            else:
+                scaled_turned = scale_turned(noise_turned)
             weights = work.tile([P, PAIR, N, PACK], BF16, bufs=1, align_bytes=64)
             add_means_gpsimd(scaled_g, weights)
             if i > 1:
                 turn_back(i - 2, hidden, False)
+            if last:
+                hidden_now = layer(i - 1, w_packed, bias, False, psum, "bank")
             add_means_turning_back(scaled_turned, weights)
             for ahead in range(len(noises_g), min(i + G_AHEAD + 1, PAIRS)):
                 noises_g.append(regroup_noise(noises[ahead], together))
@@ -428,11 +436,12 @@ def tile_bnn_pb_kernel(tc, h0, wm1, wv1, bm1, bv1, we1, be1, out):
             for ahead in range(turned_pairs, min(i + H_AHEAD + 1, PAIRS)):
                 turn_activations(ahead)
                 turned_pairs = ahead + 1
-            last_packed = new_packed() if i + 1 == PAIRS else None
             for j in range(PAIR):
                 add_means(scaled_v, weights, j)
-                if i + 1 == PAIRS:
-                    quantise_weights(weights, last_packed, slice(j, j + 1))
-            hidden = layer(i - 1, w_packed, bias, False)
-        turn_back(PAIRS - 2, hidden, False)
-        turn_back(PAIRS - 1, layer(PAIRS - 1, last_packed, bias, True), True)
+            hidden = hidden_now if last else layer(i - 1, w_packed, bias, False, psum, "bank")
+        last_packed = new_packed()
+        for j in range(PAIR):
+            quantise_weights(weights, last_packed, slice(j, j + 1))
+        last_hidden = layer(PAIRS - 1, last_packed, bias, True, psum_turn, "turn")
+        turn_back(PAIRS - 2, hidden, True)
+        turn_back(PAIRS - 1, last_hidden, True)

@@ -20,13 +20,14 @@ PACK = 4
 SLICES = N // P
 PAIR = 2
 PAIRS = SAMPLES // PAIR
-G_COLS = 128
+G_COLS = 136
 R_COLS = 128
 V_COLS = N - G_COLS - R_COLS
 H_BATCHES = ((0, 1), (1, 1), (2, 2), (4, 4), (8, 4), (12, 4))
 N_AHEAD = 3
 G_AHEAD = 2
 H_AHEAD = 4
+WARM_UP = 6
 RUN = 4
 V_RUNS = V_COLS // RUN
 BANK_RUNS = 512 // (PACK * RUN)
@@ -86,6 +87,12 @@ def tile_bnn_pb_kernel(tc, h0, wm1, wv1, bm1, bv1, we1, be1, out):
 
         bias_stat_rows = const.tile([P, P], BF16)
         nc.vector.memset(bias_stat_rows[:], 0.0)
+
+        zeros = const.tile([P, 4 * P], BF16)
+        nc.vector.memset(zeros[:], 0.0)
+        unread = psum.tile([P, 4 * P], F32, tag="bank")
+        for i in range(WARM_UP):
+            nc.tensor.matmul(out=unread[:], lhsT=zeros[:, 0:P], rhs=zeros[:], start=True, stop=True)
 
         logvar_rows = const.tile([P, PACK, N], BF16)
         nc.sync.dma_start(out=logvar_rows[:], in_=wv1.rearrange("(p t) n -> p t n", t=PACK))
@@ -409,10 +416,10 @@ def tile_bnn_pb_kernel(tc, h0, wm1, wv1, bm1, bv1, we1, be1, out):
                 load_activations(ahead)
             scaled_g = scale_gpsimd(noises_g[i], together)
             scaled_v = work.tile([P, V_RUNS, PAIR, PACK, RUN], F32)
+            last = i + 1 == PAIRS
             for c0, runs, bank in sigma_banks:
                 scale(noises[i], scaled_v, slice(0, PAIR), c0, runs, bank[:, 0:runs, :, :])
-            last = i + 1 == PAIRS
-            if i == 1:
+            if i == 1 or last:
                 scaled_turned = scale_turned(noise_turned)
             if batch_of[i - 1][0] == i - 1:
                 quantise_activations(i - 1)
@@ -420,15 +427,15 @@ def tile_bnn_pb_kernel(tc, h0, wm1, wv1, bm1, bv1, we1, be1, out):
             quantise_weights(weights, w_packed, slice(0, PAIR))
             if i == 1:
                 bias = make_bias()
-            else:
+            elif not last:
                 scaled_turned = scale_turned(noise_turned)
             weights = work.tile([P, PAIR, N, PACK], BF16, bufs=1, align_bytes=64)
             add_means_gpsimd(scaled_g, weights)
             if i > 1:
                 turn_back(i - 2, hidden, False)
+            add_means_turning_back(scaled_turned, weights)
             if last:
                 hidden_now = layer(i - 1, w_packed, bias, False, psum, "bank")
-            add_means_turning_back(scaled_turned, weights)
             for ahead in range(len(noises_g), min(i + G_AHEAD + 1, PAIRS)):
                 noises_g.append(regroup_noise(noises[ahead], together))
             if i + 1 < PAIRS:
@@ -442,6 +449,6 @@ def tile_bnn_pb_kernel(tc, h0, wm1, wv1, bm1, bv1, we1, be1, out):
         last_packed = new_packed()
         for j in range(PAIR):
             quantise_weights(weights, last_packed, slice(j, j + 1))
-        last_hidden = layer(PAIRS - 1, last_packed, bias, True, psum_turn, "turn")
         turn_back(PAIRS - 2, hidden, True)
+        last_hidden = layer(PAIRS - 1, last_packed, bias, True, psum_turn, "turn")
         turn_back(PAIRS - 1, last_hidden, True)

from contextlib import ExitStack

import concourse.mybir as mybir
from concourse.masks import make_identity

BF16 = mybir.dt.bfloat16
F32 = mybir.dt.float32
U32 = mybir.dt.uint32
U8 = mybir.dt.uint8
FP8X4 = mybir.dt.float8_e4m3fn_x4
ACT = mybir.ActivationFunctionType
ALU = mybir.AluOpType

SAMPLES = 32
ROWS = 128
K = 512
N = 512
P = 128
PACK = 4
SLICES = N // P
PAIR = 2
PAIRS = SAMPLES // PAIR
G_COLS = 136
R_COLS = 128
V_COLS = N - G_COLS - R_COLS
H_BATCHES = ((0, 1), (1, 1), (2, 2), (4, 4), (8, 4), (12, 4))
N_AHEAD = 3
G_AHEAD = 2
H_AHEAD = 4
WARM_UP = 6
RUN = 4
V_RUNS = V_COLS // RUN
BANK_RUNS = 512 // (PACK * RUN)

FLOPS = 2 * SAMPLES * ROWS * K * N


def tile_bnn_pb_kernel(tc, h0, wm1, wv1, bm1, bv1, we1, be1, out):
    nc = tc.nc
    with ExitStack() as ctx:
        ctx.enter_context(tc.manual_schedule())
        const = ctx.enter_context(tc.tile_pool(name="const", bufs=1))
        loads = ctx.enter_context(tc.tile_pool(name="loads", bufs=4))
        work = ctx.enter_context(tc.tile_pool(name="work", bufs=2))
        packed = ctx.enter_context(tc.tile_pool(name="packed", bufs=4))
        results = ctx.enter_context(tc.tile_pool(name="results", bufs=2))
        psum_const = ctx.enter_context(tc.psum_pool(name="psum_const", bufs=1))
        psum = ctx.enter_context(tc.psum_pool(name="psum", bufs=3))
        psum_turn = ctx.enter_context(tc.psum_pool(name="psum_turn", bufs=2))

        ident_f32 = const.tile([P, P], F32)
        make_identity(nc, ident_f32[:])
        ident_bf16 = const.tile([P, P], BF16)
        make_identity(nc, ident_bf16[:])

        v_cols = slice(0, V_COLS)
        r_cols = slice(V_COLS, V_COLS + R_COLS)
        g_cols = slice(V_COLS + R_COLS, N)
        v_banks = [(c0, min(BANK_RUNS, V_RUNS - c0)) for c0 in range(0, V_RUNS, BANK_RUNS)]

        def samples_of(i):
            return slice(i * PAIR, (i + 1) * PAIR)

        noises = []
        activations = []

        def load_noise(i, calls):
            noise = loads.tile([P, PAIR, PACK, N], BF16, bufs=5)
            noises.append(noise)
            return [
                (noise[:, part, :, :], we1[i * PAIR + part.start : i * PAIR + part.stop])
                for part in split_pair(calls)
            ]

        def split_pair(calls):
            per_call = PAIR // calls
            return [slice(j, j + per_call) for j in range(0, PAIR, per_call)]

        def start_load(half):
            to, rows = half
            nc.sync.dma_start(out=to, in_=rows.rearrange("s (p t) n -> p s t n", t=PACK))

        def load_activations(i):
            acts = loads.tile([P, PAIR, K], BF16)
            nc.sync.dma_start(out=acts[:], in_=h0[samples_of(i)].rearrange("s r k -> r s k"))
            activations.append(acts)

        bias_stat_rows = const.tile([P, P], BF16)
        nc.vector.memset(bias_stat_rows[:], 0.0)

        zeros = const.tile([P, 4 * P], BF16)
        nc.vector.memset(zeros[:], 0.0)
        unread = psum.tile([P, 4 * P], F32, tag="bank")
        for i in range(WARM_UP):
            nc.tensor.matmul(out=unread[:], lhsT=zeros[:, 0:P], rhs=zeros[:], start=True, stop=True)

        logvar_rows = const.tile([P, PACK, N], BF16)
        nc.sync.dma_start(out=logvar_rows[:], in_=wv1.rearrange("(p t) n -> p t n", t=PACK))
        first_halves = load_noise(0, PAIR)
        start_load(first_halves[0])
        start_load(first_halves[1])
        mean_rows = const.tile([P, PACK, N], BF16)
        nc.sync.dma_start(out=mean_rows[:], in_=wm1.rearrange("(p t) n -> p t n", t=PACK))
        start_load(load_noise(1, 1)[0])
        load_activations(0)
        bias_noise_rows = const.tile([P, P], BF16)
        nc.sync.dma_start(out=bias_noise_rows[:], in_=be1.rearrange("s o (c l) -> (s o c) l", l=P))
        nc.sync.dma_start(out=bias_stat_rows[0:SLICES, :], in_=bv1.rearrange("(c l) -> c l", l=P))
        nc.sync.dma_start(
            out=bias_stat_rows[SLICES : 2 * SLICES, :], in_=bm1.rearrange("(c l) -> c l", l=P)
        )
        load_activations(1)
        for i in range(2, N_AHEAD):
            start_load(load_noise(i, 1)[0])
            load_activations(i)

        sigma_v = const.tile([P, V_RUNS, PACK, RUN], F32)
        for c0, runs in v_banks:
            nc.scalar.activation(
                out=sigma_v[:, c0 : c0 + runs, :, :],
                in_=logvar_rows[:, :, c0 * RUN : (c0 + runs) * RUN].rearrange(
                    "p t (c i) -> p c t i", i=RUN
                ),
                func=ACT.Exp,
                scale=0.5,
            )
        sigma_g = const.tile([P, G_COLS, PACK], F32)
        nc.scalar.activation(
            out=sigma_g[:],
            in_=logvar_rows[:, :, g_cols].rearrange("p t n -> p n t"),
            func=ACT.Exp,
            scale=0.5,
        )

        sigma_banks = []

        def fill_sigma_bank(c0, runs):
            bank = psum_const.tile([P, BANK_RUNS, PACK, RUN], F32, name="sigma_bank%d" % c0)
            nc.tensor.matmul(
                out=bank[:, 0:runs, :, :].rearrange("p c t i -> p (c t i)"),
                lhsT=ident_f32[:],
                rhs=sigma_v[:, c0 : c0 + runs, :, :].rearrange("p c t i -> p (c t i)"),
                start=True,
                stop=True,
            )
            sigma_banks.append((c0, runs, bank))

        batch_of = {}
        for first, pairs in H_BATCHES:
            for i in range(first, first + pairs):
                batch_of[i] = (first, pairs)
        h_grouped = {}
        h_packed = {}

        def turn_activations(i):
            first, pairs = batch_of[i]
            act_words = activations[i][:].bitcast(F32).rearrange("r s (q u) -> r s u q", u=2)
            turned = psum.tile([P, PAIR, 2, ROWS], F32, tag="bank")
            for j in range(PAIR):
                for u in range(2):
                    nc.tensor.transpose(turned[:, j, u, :], act_words[:, j, u, :], ident_f32[:])
            if i == first:
                grouped = work.tile([P, pairs * PAIR, ROWS, PACK], BF16, bufs=3, align_bytes=64)
                h_grouped[first] = grouped
            nc.scalar.copy(
                out=h_grouped[first][:, samples_of(i - first), :, :].bitcast(F32),
                in_=turned[:].rearrange("q s u r -> q s r u"),
            )

        def quantise_activations(first):
            pairs = batch_of[first][1]
            h_codes = packed.tile([P, pairs * PAIR, ROWS], U32, align_bytes=64)
            h_scales = packed.tile([P, pairs * PAIR, ROWS], U8, align_bytes=64)
            nc.vector.quantize_mx(
                out=h_codes[:].rearrange("q s r -> q (s r)").bitcast(FP8X4),
                scales=h_scales[:].rearrange("q s r -> q (s r)"),
                in_=h_grouped[first][:].rearrange("q s r t -> q (s r t)"),
            )
            h_packed[first] = (h_codes, h_scales)

        def new_packed():
            w_codes = packed.tile([P, PAIR, N], U32, align_bytes=64)
            w_scales = packed.tile([P, PAIR, N], U8, align_bytes=64)
            return w_codes, w_scales

        def quantise_weights(weights, w_packed, part):
            w_codes, w_scales = w_packed
            nc.vector.quantize_mx(
                out=w_codes[:, part, :].rearrange("p s n -> p (s n)").bitcast(FP8X4),
                scales=w_scales[:, part, :].rearrange("p s n -> p (s n)"),
                in_=weights[:, part, :, :].rearrange("p s n t -> p (s n t)"),
            )

        def layer(i, w_packed, bias, vector_helps, pool, tag):
            w_codes, w_scales = w_packed
            first = batch_of[i][0]
            h_codes, h_scales = h_packed[first]
            h_at = (i - first) * PAIR
            products = []
            for j in range(PAIR):
                product = pool.tile([P, SLICES, ROWS], F32, tag=tag)
                for c in range(SLICES):
                    cols = slice(c * P, (c + 1) * P)
                    nc.tensor.matmul_mx(
                        out=product[:, c, :],
                        lhsT=w_codes[:, j, cols].bitcast(FP8X4),
                        lhsT_scale=w_scales[:, j, cols],
                        rhs=h_codes[:, h_at + j, :].bitcast(FP8X4),
                        rhs_scale=h_scales[:, h_at + j, :],
                        start=True,
                        stop=True,
                    )
                products.append(product)
            hidden = results.tile([P, PAIR, SLICES, ROWS], F32)
            for j in range(PAIR):
                for c in range(SLICES):
                    if vector_helps and j == PAIR - 1:
                        nc.vector.tensor_scalar(
                            out=hidden[:, j, c, :],
                            in0=products[j][:, c, :],
                            scalar1=bias[:, i * PAIR + j, c : c + 1],
                            scalar2=0.0,
                            op0=ALU.add,
                            op1=ALU.max,
                        )
                    else:
                        nc.scalar.activation(
                            out=hidden[:, j, c, :],
                            in_=products[j][:, c, :],
                            func=ACT.Relu,
                            bias=bias[:, i * PAIR + j, c : c + 1],
                            scale=1.0,
                        )
            return hidden

        def turn_back(i, hidden, vector_helps):
            backs = []
            for j in range(PAIR):
                back = psum.tile([P, SLICES, P], F32, tag="bank")
                for c in range(SLICES):
                    nc.tensor.transpose(back[:, c, :], hidden[:, j, c, :], ident_f32[:])
                backs.append(back)
            result = results.tile([P, PAIR, N], F32)
            for j in range(PAIR):
                if vector_helps and j == PAIR - 1:
                    nc.vector.tensor_copy(out=result[:, j, :], in_=backs[j][:].rearrange("r c l -> r (c l)"))
                    nc.sync.dma_start(out=out[i * PAIR + j], in_=result[:, j, :])
                else:
                    nc.scalar.copy(out=result[:, j, :], in_=backs[j][:].rearrange("r c l -> r (c l)"))
                    nc.sync.dma_start(out=out[i * PAIR + j], in_=result[:, j, :])

        def regroup_noise(noise, parts):
            noise_g = work.tile([P, PAIR, G_COLS, PACK], BF16, bufs=4)
            for part in parts:
                nc.scalar.copy(
                    out=noise_g[:, part, :, :],
                    in_=noise[:, part, :, g_cols].rearrange("p s t n -> p s n t"),
                )
            return noise_g

        def scale_gpsimd(noise_g, parts):
            scaled_g = work.tile([P, PAIR, G_COLS, PACK], F32)
            for part in parts:
                samples = part.stop - part.start
                nc.gpsimd.tensor_tensor(
                    out=scaled_g[:, part, :, :],
                    in0=noise_g[:, part, :, :],
                    in1=sigma_g[:].unsqueeze(1).to_broadcast([P, samples, G_COLS, PACK]),
                    op=ALU.mult,
                )
            return scaled_g

        def add_means_gpsimd(scaled_g, weights):
            nc.gpsimd.tensor_tensor(
                out=weights[:, :, g_cols, :],
                in0=scaled_g[:],
                in1=mean_g[:].unsqueeze(1).to_broadcast([P, PAIR, G_COLS, PACK]),
                op=ALU.add,
            )

        def turn_noise(noise):
            noise_turned = psum_turn.tile([P, PAIR, PACK, P], BF16, tag="turn")
            for j in range(PAIR):
                for t in range(PACK):
                    nc.tensor.transpose(noise_turned[:, j, t, :], noise[:, j, t, r_cols], ident_bf16[:])
            return noise_turned

        def scale_turned(noise_turned):
            scaled_turned = work.tile([P, PAIR, PACK, P], F32)
            nc.vector.tensor_tensor(
                out=scaled_turned[:],
                in0=noise_turned[:],
                in1=sigma_turned[:].unsqueeze(1).to_broadcast([P, PAIR, PACK, P]),
                op=ALU.mult,
            )
            return scaled_turned

        def add_means_turning_back(scaled_turned, weights):
            for j in range(PAIR):
                summed = psum_turn.tile([P, PACK, P], F32, tag="turn")
                for t in range(PACK):
                    nc.tensor.matmul(
                        out=summed[:, t, :],
                        lhsT=mean_turned[:, t, :],
                        rhs=ident_f32[:],
                        is_transpose=True,
                        start=True,
                        stop=False,
                    )
                    nc.tensor.matmul(
                        out=summed[:, t, :],
                        lhsT=scaled_turned[:, j, t, :],
                        rhs=ident_f32[:],
                        is_transpose=True,
                        start=False,
                        stop=True,
                    )
                nc.scalar.copy(
                    out=weights[:, j, r_cols, :], in_=summed[:].rearrange("p t n -> p n t")
                )

        def scale(noise, scaled_v, part, c0, runs, sigma):
            samples = part.stop - part.start
            nc.vector.tensor_tensor(
                out=scaled_v[:, c0 : c0 + runs, part, :, :],
                in0=noise[:, part, :, c0 * RUN : (c0 + runs) * RUN].rearrange(
                    "p s t (c i) -> p c s t i", i=RUN
                ),
                in1=sigma.unsqueeze(2).to_broadcast([P, runs, samples, PACK, RUN]),
                op=ALU.mult,
            )

        def add_means(scaled_v, weights, j):
            nc.vector.tensor_tensor(
                out=weights[:, j, v_cols, :].rearrange("p (c i) t -> p c t i", i=RUN),
                in0=scaled_v[:, :, j, :, :],
                in1=mean_bank[:, 0:V_RUNS, :, :],
                op=ALU.add,
            )

        def make_bias():
            bias_noise = psum.tile([P, P], BF16, tag="bank")
            nc.tensor.transpose(bias_noise[:], bias_noise_rows[:], ident_bf16[:])
            bias_stat = psum.tile([P, P], BF16, tag="bank")
            nc.tensor.transpose(bias_stat[:], bias_stat_rows[:], ident_bf16[:])
            bias_sigma = const.tile([P, SLICES], F32)
            nc.scalar.activation(out=bias_sigma[:], in_=bias_stat[:, 0:SLICES], func=ACT.Exp, scale=0.5)
            bias_scaled = const.tile([P, SAMPLES, SLICES], F32)
            nc.vector.tensor_tensor(
                out=bias_scaled[:],
                in0=bias_noise[:].rearrange("l (s c) -> l s c", c=SLICES),
                in1=bias_sigma[:].unsqueeze(1).to_broadcast([P, SAMPLES, SLICES]),
                op=ALU.mult,
            )
            bias = const.tile([P, SAMPLES, SLICES], F32)
            nc.vector.tensor_tensor(
                out=bias[:],
                in0=bias_scaled[:],
                in1=bias_stat[:, SLICES : 2 * SLICES].unsqueeze(1).to_broadcast([P, SAMPLES, SLICES]),
                op=ALU.add,
            )
            return bias

        one_by_one = split_pair(PAIR)
        together = split_pair(1)
        weights = work.tile([P, PAIR, N, PACK], BF16, bufs=1, align_bytes=64)
        logvar_turned = psum.tile([P, PACK, P], BF16, tag="bank")
        for t in range(PACK):
            nc.tensor.transpose(logvar_turned[:, t, :], logvar_rows[:, t, r_cols], ident_bf16[:])
        sigma_turned = const.tile([P, PACK, P], F32)
        nc.scalar.activation(out=sigma_turned[:], in_=logvar_turned[:], func=ACT.Exp, scale=0.5)
        noises_g = [regroup_noise(noises[0], one_by_one)]
        mean_g = const.tile([P, G_COLS, PACK], BF16)
        nc.scalar.copy(out=mean_g[:], in_=mean_rows[:, :, g_cols].rearrange("p t n -> p n t"))
        add_means_gpsimd(scale_gpsimd(noises_g[0], one_by_one), weights)

        fill_sigma_bank(*v_banks[0])
        scaled_v = work.tile([P, V_RUNS, PAIR, PACK, RUN], F32)
        for part in one_by_one:
            for c0, runs in v_banks:
                scale(noises[0], scaled_v, part, c0, runs, sigma_v[:, c0 : c0 + runs, :, :])
        noise_turned = turn_noise(noises[0])
        mean_bank = psum_const.tile([P, 2 * BANK_RUNS, PACK, RUN], BF16)
        for c0, runs in v_banks:
            nc.tensor.matmul(
                out=mean_bank[:, c0 : c0 + runs, :, :],
                lhsT=ident_bf16[:],
                rhs=mean_rows[:, :, c0 * RUN : (c0 + runs) * RUN].rearrange(
                    "p t (c i) -> p c t i", i=RUN
                ),
                start=True,
                stop=True,
            )
        mean_turned_bf16 = psum.tile([P, PACK, P], BF16, tag="bank")
        for t in range(PACK):
            nc.tensor.transpose(mean_turned_bf16[:, t, :], mean_rows[:, t, r_cols], ident_bf16[:])
        mean_turned = const.tile([P, PACK, P], F32)
        nc.scalar.copy(out=mean_turned[:], in_=mean_turned_bf16[:])
        noises_g.append(regroup_noise(noises[1], together))
        fill_sigma_bank(*v_banks[1])
        add_means_turning_back(scale_turned(noise_turned), weights)
        for j in range(PAIR):
            add_means(scaled_v, weights, j)
        noise_turned = turn_noise(noises[1])
        turn_activations(0)

        turn_activations(1)
        noises_g.append(regroup_noise(noises[2], together))

        turned_pairs = 2
        hidden = None
        for i in range(1, PAIRS):
            for ahead in range(len(noises), min(i + N_AHEAD + 1, PAIRS)):
                start_load(load_noise(ahead, 1)[0])
            for ahead in range(len(activations), min(i + H_AHEAD + 1, PAIRS)):
                load_activations(ahead)
            scaled_g = scale_gpsimd(noises_g[i], together)
            scaled_v = work.tile([P, V_RUNS, PAIR, PACK, RUN], F32)
            last = i + 1 == PAIRS
            for c0, runs, bank in sigma_banks:
                scale(noises[i], scaled_v, slice(0, PAIR), c0, runs, bank[:, 0:runs, :, :])
            if i == 1 or last:
                scaled_turned = scale_turned(noise_turned)
            if batch_of[i - 1][0] == i - 1:
                quantise_activations(i - 1)
            w_packed = new_packed()
            quantise_weights(weights, w_packed, slice(0, PAIR))
            if i == 1:
                bias = make_bias()
            elif not last:
                scaled_turned = scale_turned(noise_turned)
            weights = work.tile([P, PAIR, N, PACK], BF16, bufs=1, align_bytes=64)
            add_means_gpsimd(scaled_g, weights)
            if i > 1:
                turn_back(i - 2, hidden, False)
            add_means_turning_back(scaled_turned, weights)
            if last:
                hidden_now = layer(i - 1, w_packed, bias, False, psum, "bank")
            for ahead in range(len(noises_g), min(i + G_AHEAD + 1, PAIRS)):
                noises_g.append(regroup_noise(noises[ahead], together))
            if i + 1 < PAIRS:
                noise_turned = turn_noise(noises[i + 1])
            for ahead in range(turned_pairs, min(i + H_AHEAD + 1, PAIRS)):
                turn_activations(ahead)
                turned_pairs = ahead + 1
            for j in range(PAIR):
                add_means(scaled_v, weights, j)
            hidden = hidden_now if last else layer(i - 1, w_packed, bias, False, psum, "bank")
        last_packed = new_packed()
        for j in range(PAIR):
            quantise_weights(weights, last_packed, slice(j, j + 1))
        turn_back(PAIRS - 2, hidden, True)
        last_hidden = layer(PAIRS - 1, last_packed, bias, True, psum_turn, "turn")
        turn_back(PAIRS - 1, last_hidden, True)
